import numpy as np
import ml_dtypes


def mxq(x, axis, fmt="e4m3"):
    dtype, down = {"e4m3": (ml_dtypes.float8_e4m3fn, 7), "e5m2": (ml_dtypes.float8_e5m2, 14)}[fmt]
    v = np.moveaxis(np.asarray(x, np.float32).astype(ml_dtypes.bfloat16).astype(np.float64), axis, -1)
    blocks = v.reshape(v.shape[:-1] + (-1, 32))
    amax = np.abs(blocks).max(-1, keepdims=True)
    byte = np.maximum(np.where(amax > 0, np.frexp(amax)[1] - 1 + 127, 0) - down, 1)
    scale = np.exp2(byte - 127.0)
    codes = (blocks / scale).astype(np.float32).astype(dtype).astype(np.float64)
    return np.moveaxis((codes * scale).reshape(v.shape), -1, axis)


WIDE = False


def mx_kscale(k):
    if not WIDE:
        return np.ones(k)
    levels = np.array([10, -10, 5, -5, 0])
    a = np.random.permutation(np.resize(levels, k // 512 * 4)).reshape(k // 512, 4)
    idx = np.arange(k)
    return np.exp2(a[idx // 512, idx % 128 // 32])


BF16 = ml_dtypes.bfloat16


def bf(x):
    return np.asarray(x, np.float32).astype(BF16)


def f64(x):
    return np.asarray(x).astype(np.float64)


N, D = 1024, 1024


def adjacent_mat(adj):
    adj = adj + np.eye(adj.shape[0])
    deg = np.sum(adj, axis=1)
    dinv = np.where(deg > 0, deg ** -0.5, 0.0)
    return dinv[:, None] * adj * dinv[None, :]


def setup_inputs():
    s = mx_kscale(N)
    u = s * s
    kap = (1.0 / s.min()) ** 4
    g = u.mean()
    return {"x": bf(np.random.standard_normal((N, D)) / s[:, None]),
            "Coefficient2": bf(np.random.standard_normal((N, N)) * (0.15 * np.sqrt(N)) * g / s),
            "A": bf(np.random.uniform(size=(N, N)) * kap * u[:, None] * u)}


def reference(x, Coefficient2, A):
    A_c = f64(A)
    adj = adjacent_mat((A_c + A_c.T) * 0.5)
    y = mxq(f64(Coefficient2), 1, "e4m3") @ mxq(adj, 0, "e4m3")
    y = mxq(y, 1, "e4m3") @ mxq(f64(x), 0, "e4m3")
    return y

@@ -1,0 +1,293 @@
+from contextlib import ExitStack
+
+import concourse.mybir as mybir
+from concourse.masks import make_identity
+
+F32 = mybir.dt.float32
+BF16 = mybir.dt.bfloat16
+U32 = mybir.dt.uint32
+U8 = mybir.dt.uint8
+FP8X4 = mybir.dt.float8_e4m3fn_x4
+ALU = mybir.AluOpType
+ACT = mybir.ActivationFunctionType
+AX = mybir.AxisListType
+
+P = 128
+N = 1024
+FLOPS = 2 * 2 * N * N * N
+TINY = 2.0 ** -100
+
+
+def tile_selfexpression2_kernel(tc, x, Coefficient2, A, out):
+    nc = tc.nc
+    with ExitStack() as ctx:
+        keep = ctx.enter_context(tc.tile_pool(name="keep", bufs=1))
+        stage = ctx.enter_context(tc.tile_pool(name="stage", bufs=4))
+        psum = ctx.enter_context(tc.psum_pool(name="psum", bufs=1))
+
+        def bank(i, name):
+            return psum.tile([P, 512], F32, tag="bank%d" % i, name=name)
+
+        def bank_bf(i, name):
+            return psum.tile([P, 1024], BF16, tag="bank%d" % i, name=name)
+
+        ident_f = keep.tile([P, P], F32, name="ident_f")
+        make_identity(nc, ident_f[:])
+        ident_b = keep.tile([P, P], BF16, name="ident_b")
+        make_identity(nc, ident_b[:])
+        two_eye = keep.tile([P, P], BF16, name="two_eye")
+        nc.gpsimd.tensor_scalar(out=two_eye[:], in0=ident_f[:], scalar1=2.0, scalar2=0.0,
+                                op0=ALU.mult, op1=ALU.add)
+        ones_b = keep.tile([P, 2], BF16, name="ones_b")
+        nc.vector.memset(ones_b[:], 1.0)
+        warm = keep.tile([P, 1], F32, name="warm")
+        nc.vector.memset(warm[:], 1.0)
+        nc.scalar.activation(out=warm[:], in_=warm[:], func=ACT.Sqrt)
+
+        a_sb = keep.tile([P, 4, 2, N], BF16, name="a_sb")
+        for v in range(4):
+            nc.sync.dma_start(out=a_sb[:, v, :, :],
+                              in_=A[256 * v:256 * (v + 1), :].rearrange("(p e) c -> p e c", e=2))
+        c_sb = keep.tile([P, 8, N], BF16, name="c_sb")
+        for h in range(4):
+            nc.sync.dma_start(out=c_sb[:, 2 * h:2 * h + 2, :],
+                              in_=Coefficient2[256 * h:256 * (h + 1), :].rearrange("(b p) k -> p b k", p=P))
+        x_sb = keep.tile([P, 2, 4, N], BF16, name="x_sb")
+        for v in range(4):
+            nc.sync.dma_start(out=x_sb[:, v // 2, 2 * (v % 2):2 * (v % 2) + 2, :],
+                              in_=x[256 * v:256 * (v + 1), :].rearrange("(p e) d -> p e d", e=2))
+
+        adjn = keep.tile([P, 8, N], BF16, name="adjn")
+        dj_sb = keep.tile([P, N], F32, name="dj_sb")
+        junk = keep.tile([P, N], BF16, name="junk")
+        adj_g = keep.tile([P, 2, N, 4], BF16, name="adj_g", align_bytes=64)
+        c_g = keep.tile([P, 2, N, 4], BF16, name="c_g", align_bytes=64)
+        x_g = keep.tile([P, 2, N, 4], BF16, name="x_g", align_bytes=64)
+        y_g = keep.tile([P, 2, N, 4], BF16, name="y_g", align_bytes=64)
+        adj_c = keep.tile([P, 2, N], U32, name="adj_c", align_bytes=64)
+        c_c = keep.tile([P, 2, N], U32, name="c_c", align_bytes=64)
+        x_c = keep.tile([P, 2, N], U32, name="x_c", align_bytes=64)
+        y_c = keep.tile([P, 2, N], U32, name="y_c", align_bytes=64)
+        adj_s = keep.tile([P, 2, N], U8, name="adj_s", align_bytes=64)
+        c_s = keep.tile([P, 2, N], U8, name="c_s", align_bytes=64)
+        x_s = keep.tile([P, 2, N], U8, name="x_s", align_bytes=64)
+        y_s = keep.tile([P, 2, N], U8, name="y_s", align_bytes=64)
+
+        def quantise(grouped, codes, scales, g, c0, cols):
+            nc.vector.quantize_mx(
+                out=codes[:, g, c0:c0 + cols].bitcast(FP8X4),
+                scales=scales[:, g, c0:c0 + cols],
+                in_=grouped[:, g, c0:c0 + cols, :].rearrange("p j t -> p (j t)"),
+            )
+
+        def regroup(eng_copy, dst, src):
+            eng_copy(out=dst.rearrange("p (c i) t -> p c t i", i=4),
+                     in_=src.rearrange("p t (c i) -> p c t i", i=4))
+
+        def a_cols(v, e, vc, ec):
+            return a_sb[:, v, e, 256 * vc + ec:256 * vc + 256:2]
+
+        rs = keep.tile([P, 16], F32, name="rs")
+        colp = bank(7, "colp")
+        for w in range(4):
+            nc.vector.tensor_reduce(out=rs[:, w:w + 1], in_=a_sb[:, w, 0, :], axis=AX.X, op=ALU.add)
+            nc.scalar.activation(out=junk[:], in_=a_sb[:, w, 1, :], func=ACT.Copy,
+                                 accum_out=rs[:, 8 + w:9 + w])
+            for e in range(2):
+                for v in range(4):
+                    i0 = ((w * 2 + e) * 4 + v) * 2
+                    for ew in range(2):
+                        nc.tensor.matmul(colp[:, i0:i0 + 2], lhsT=a_cols(w, ew, v, e), rhs=ones_b[:],
+                                         start=(ew == 0), stop=(ew == 1))
+
+        tiles = [(0, 0, 0), (0, 1, 0), (1, 0, 0), (1, 1, 0), (2, 0, 2), (2, 1, 0), (3, 0, 2), (3, 1, 0),
+                 (4, 1, 0), (5, 1, 0), (6, 1, 2), (7, 1, 2)]
+        s2p = {}
+
+        def add_tile(n):
+            a, G, t0 = tiles[n]
+            v, e = a // 2, a % 2
+            tl = bank(n % 4, "s2p")
+            s2p[n] = tl
+            for t2 in range(t0, 4):
+                c = 4 * G + t2
+                vc, ec = c // 2, c % 2
+                o = tl[:, 128 * t2:128 * (t2 + 1)]
+                nc.tensor.matmul(o, lhsT=ident_b[:], rhs=a_cols(v, e, vc, ec), start=True, stop=False)
+                nc.tensor.matmul(o, lhsT=a_cols(vc, ec, v, e), rhs=ident_b[:], start=False, stop=(c != a))
+                if c == a:
+                    nc.tensor.matmul(o, lhsT=ident_b[:], rhs=two_eye[:], start=False, stop=True)
+
+        for n in range(4):
+            add_tile(n)
+
+        c_gw = c_g[:].bitcast(F32)
+        for ib in range(8):
+            ctp = bank(5 + ib % 2, "ctp")
+            for vv in range(4):
+                nc.tensor.transpose(
+                    ctp[:, 128 * vv:128 * (vv + 1)],
+                    c_sb[:, ib, :].bitcast(F32)[:, 128 * vv:128 * (vv + 1)],
+                    ident_f[:])
+            nc.scalar.copy(out=c_gw[:, :, 128 * ib:128 * (ib + 1), :],
+                           in_=ctp[:].rearrange("p (g u i) -> p g i u", g=2, u=2))
+
+        def small(name):
+            return keep.tile([P, 8], F32, name=name)
+
+        cs = small("cs")
+        nc.vector.tensor_reduce(
+            out=cs[:], in_=colp[:, 0:64].rearrange("p (w a n) -> p a n w", w=4, n=2)[:, :, 0, :],
+            axis=AX.X, op=ALU.add)
+        d = small("d")
+        nc.vector.scalar_tensor_tensor(
+            out=d[:].rearrange("p (e v) -> p e v", e=2),
+            in0=rs[:].rearrange("p (e c) -> p e c", e=2)[:, :, 0:4], scalar=2.0,
+            in1=cs[:].rearrange("p (e v) -> p e v", e=2), op0=ALU.add, op1=ALU.add)
+        dm = small("dm")
+        nc.vector.tensor_scalar_max(out=dm[:], in0=d[:], scalar1=TINY)
+        mask = small("mask")
+        nc.vector.tensor_single_scalar(out=mask[:], in_=d[:], scalar=0.0, op=ALU.is_gt)
+        rt = small("rt")
+        nc.scalar.activation(out=rt[:], in_=dm[:], func=ACT.Sqrt)
+        y0 = small("y0")
+        nc.vector.reciprocal(out=y0[:], in_=rt[:])
+        t1 = small("t1")
+        nc.vector.tensor_mul(out=t1[:], in0=dm[:], in1=y0[:])
+        t2_ = small("t2_")
+        nc.vector.scalar_tensor_tensor(out=t2_[:], in0=t1[:], scalar=-0.5, in1=y0[:], op0=ALU.mult, op1=ALU.mult)
+        y1 = small("y1")
+        nc.vector.scalar_tensor_tensor(out=y1[:], in0=t2_[:], scalar=1.5, in1=y0[:], op0=ALU.add, op1=ALU.mult)
+        t3 = small("t3")
+        nc.vector.tensor_mul(out=t3[:], in0=dm[:], in1=y1[:])
+        y1m = small("y1m")
+        nc.vector.tensor_mul(out=y1m[:], in0=y1[:], in1=mask[:])
+        t4 = small("t4")
+        nc.vector.scalar_tensor_tensor(out=t4[:], in0=t3[:], scalar=-0.5, in1=y1[:], op0=ALU.mult, op1=ALU.mult)
+        dinv = small("dinv")
+        nc.vector.scalar_tensor_tensor(out=dinv[:], in0=t4[:], scalar=1.5, in1=y1m[:], op0=ALU.add, op1=ALU.mult)
+
+        def dcol(a):
+            i = 4 * (a % 2) + a // 2
+            return dinv[:, i:i + 1]
+
+        rowp = [bank(7, "rowp0"), bank(4, "rowp1")]
+        for a in range(8):
+            nc.tensor.transpose(rowp[a // 4][:, 128 * (a % 4):128 * (a % 4 + 1)],
+                                dcol(a).to_broadcast([P, P]), ident_f[:])
+        nc.vector.tensor_copy(out=dj_sb[:, 0:512], in_=rowp[0][:])
+        nc.scalar.copy(out=dj_sb[:, 512:1024], in_=rowp[1][:])
+
+        for g in range(2):
+            for h in range(2):
+                quantise(c_g, c_c, c_s, g, 512 * h, 512)
+
+        def scale_tile(n):
+            a, G, t0 = tiles[n]
+            lo, hi = 512 * G + 128 * t0, 512 * (G + 1)
+            nc.vector.scalar_tensor_tensor(
+                out=adjn[:, a, lo:hi], in0=s2p[n][:, 128 * t0:512], scalar=dcol(a),
+                in1=dj_sb[:, lo:hi], op0=ALU.mult, op1=ALU.mult)
+
+        def lower_diag(g, b):
+            ld = bank_bf(b, "ld")
+            for r in range(2):
+                a = 4 * g + 2 + r
+                for cc in range(2):
+                    c = 4 * g + cc
+                    q = 2 * r + cc
+                    nc.tensor.transpose(ld[:, 128 * q:128 * (q + 1)], adjn[:, c, 128 * a:128 * (a + 1)], ident_b[:])
+            nc.scalar.copy(out=adjn[:, 4 * g + 2:4 * g + 4, 512 * g:512 * g + 256],
+                           in_=ld[:, 0:512].rearrange("p (r j) -> p r j", r=2))
+
+        def lower_off(h, b):
+            lt = bank_bf(b, "lt")
+            for cl in range(2):
+                c = 2 * h + cl
+                for t in range(4):
+                    q = 4 * cl + t
+                    nc.tensor.transpose(lt[:, 128 * q:128 * (q + 1)], adjn[:, c, 128 * (4 + t):128 * (5 + t)],
+                                        ident_b[:])
+            nc.scalar.copy(out=adj_g[:, 1, 256 * h:256 * (h + 1), :].rearrange("p (cl j) t -> p cl j t", cl=2),
+                           in_=lt[:].rearrange("p (cl t j) -> p cl j t", cl=2, t=4))
+
+        for n in range(4):
+            scale_tile(n)
+        add_tile(4)
+        add_tile(5)
+        lower_diag(0, 5)
+        lower_off(0, 6)
+        add_tile(6)
+        add_tile(7)
+        for n in range(4, 8):
+            scale_tile(n)
+        lower_off(1, 5)
+        for n in range(8, 12):
+            add_tile(n)
+        regroup(nc.vector.tensor_copy, adj_g[:, 0, 0:512, :], adjn[:, 0:4, 0:512])
+        quantise(adj_g, adj_c, adj_s, 0, 0, 512)
+        quantise(adj_g, adj_c, adj_s, 1, 0, 512)
+        regroup(nc.scalar.copy, adj_g[:, 0, 512:1024, :], adjn[:, 0:4, 512:1024])
+        for n in range(8, 12):
+            scale_tile(n)
+        lower_diag(1, 0)
+        regroup(nc.vector.tensor_copy, adj_g[:, 1, 512:1024, :], adjn[:, 4:8, 512:1024])
+        quantise(adj_g, adj_c, adj_s, 0, 512, 512)
+        quantise(adj_g, adj_c, adj_s, 1, 512, 512)
+
+        nb = [0]
+
+        def next_bank(name, banks):
+            b = banks[nb[0] % len(banks)]
+            nb[0] += 1
+            return bank(b, name)
+
+        def first_matmul(G, banks, engines):
+            for ib in range(8):
+                yp = next_bank("yp", banks)
+                for t2 in range(4):
+                    j0 = 512 * G + 128 * t2
+                    for g in range(2):
+                        nc.tensor.matmul_mx(
+                            out=yp[:, 128 * t2:128 * (t2 + 1)],
+                            lhsT=adj_c[:, g, j0:j0 + 128].bitcast(FP8X4),
+                            lhsT_scale=adj_s[:, g, j0:j0 + 128],
+                            rhs=c_c[:, g, 128 * ib:128 * (ib + 1)].bitcast(FP8X4),
+                            rhs_scale=c_s[:, g, 128 * ib:128 * (ib + 1)],
+                            start=(g == 0), stop=(g == 1))
+                engines[ib % len(engines)](
+                    out=y_g[:, G, 128 * ib:128 * (ib + 1), :],
+                    in_=yp[:].rearrange("p (t i) -> p i t", t=4))
+                if ib % 2 == 1:
+                    quantise(y_g, y_c, y_s, G, 128 * (ib - 1), 256)
+
+        first_matmul(0, [4, 5, 6, 7], [nc.scalar.copy])
+
+        for G in range(2):
+            regroup(nc.vector.tensor_copy, x_g[:, G, 0:512, :], x_sb[:, G, :, 0:512])
+            regroup(nc.scalar.copy, x_g[:, G, 512:1024, :], x_sb[:, G, :, 512:1024])
+        for G in range(2):
+            for h in range(2):
+                quantise(x_g, x_c, x_s, G, 512 * h, 512)
+
+        all_banks = [0, 1, 2, 3, 4, 5, 6, 7]
+        nb[0] = 0
+        first_matmul(1, all_banks, [nc.scalar.copy, nc.vector.tensor_copy])
+
+        for ib in range(8):
+            ost = stage.tile([P, N], F32, name="ost")
+            for h in range(2):
+                op = next_bank("op", all_banks)
+                for G in range(2):
+                    nc.tensor.matmul_mx(
+                        out=op[:],
+                        lhsT=y_c[:, G, 128 * ib:128 * (ib + 1)].bitcast(FP8X4),
+                        lhsT_scale=y_s[:, G, 128 * ib:128 * (ib + 1)],
+                        rhs=x_c[:, G, 512 * h:512 * (h + 1)].bitcast(FP8X4),
+                        rhs_scale=x_s[:, G, 512 * h:512 * (h + 1)],
+                        start=(G == 0), stop=(G == 1))
+                if h == 0:
+                    nc.vector.tensor_copy(out=ost[:, 0:512], in_=op[:])
+                else:
+                    nc.scalar.copy(out=ost[:, 512:1024], in_=op[:])
+            nc.sync.dma_start(out=out[128 * ib:128 * (ib + 1), :], in_=ost[:])

@@ -12,18 +12,24 @@ ALU = mybir.AluOpType
 ACT = mybir.ActivationFunctionType
 AX = mybir.AxisListType
 
+OST_BUFS = 16
+S2_BANKS = [0, 1, 2, 3]
+ROW1_BANK = 4
 P = 128
 N = 1024
 FLOPS = 2 * 2 * N * N * N
 TINY = 2.0 ** -100
+TILES = [(0, 0, 0), (0, 1, 0), (1, 0, 0), (1, 1, 0), (2, 0, 2), (2, 1, 0), (3, 0, 2), (3, 1, 0),
+         (4, 1, 0), (5, 1, 0), (6, 1, 0), (7, 1, 0)]
 
 
 def tile_selfexpression2_kernel(tc, x, Coefficient2, A, out):
     nc = tc.nc
     with ExitStack() as ctx:
         keep = ctx.enter_context(tc.tile_pool(name="keep", bufs=1))
-        stage = ctx.enter_context(tc.tile_pool(name="stage", bufs=4))
+        stage = ctx.enter_context(tc.tile_pool(name="stage", bufs=OST_BUFS))
         psum = ctx.enter_context(tc.psum_pool(name="psum", bufs=1))
+        ctx.enter_context(tc.manual_schedule())
 
         def bank(i, name):
             return psum.tile([P, 512], F32, tag="bank%d" % i, name=name)
@@ -32,9 +38,9 @@ def tile_selfexpression2_kernel(tc, x, Coefficient2, A, out):
             return psum.tile([P, 1024], BF16, tag="bank%d" % i, name=name)
 
         ident_f = keep.tile([P, P], F32, name="ident_f")
-        make_identity(nc, ident_f[:])
         ident_b = keep.tile([P, P], BF16, name="ident_b")
         make_identity(nc, ident_b[:])
+        make_identity(nc, ident_f[:])
         two_eye = keep.tile([P, P], BF16, name="two_eye")
         nc.gpsimd.tensor_scalar(out=two_eye[:], in0=ident_f[:], scalar1=2.0, scalar2=0.0,
                                 op0=ALU.mult, op1=ALU.add)
@@ -59,7 +65,7 @@ def tile_selfexpression2_kernel(tc, x, Coefficient2, A, out):
 
         adjn = keep.tile([P, 8, N], BF16, name="adjn")
         dj_sb = keep.tile([P, N], F32, name="dj_sb")
-        junk = keep.tile([P, N], BF16, name="junk")
+        junk = keep.tile([P, 4, N], BF16, name="junk")
         adj_g = keep.tile([P, 2, N, 4], BF16, name="adj_g", align_bytes=64)
         c_g = keep.tile([P, 2, N, 4], BF16, name="c_g", align_bytes=64)
         x_g = keep.tile([P, 2, N, 4], BF16, name="x_g", align_bytes=64)
@@ -72,6 +78,8 @@ def tile_selfexpression2_kernel(tc, x, Coefficient2, A, out):
         c_s = keep.tile([P, 2, N], U8, name="c_s", align_bytes=64)
         x_s = keep.tile([P, 2, N], U8, name="x_s", align_bytes=64)
         y_s = keep.tile([P, 2, N], U8, name="y_s", align_bytes=64)
+        V = nc.vector.tensor_copy
+        S = nc.scalar.copy
 
         def quantise(grouped, codes, scales, g, c0, cols):
             nc.vector.quantize_mx(
@@ -88,11 +96,17 @@ def tile_selfexpression2_kernel(tc, x, Coefficient2, A, out):
             return a_sb[:, v, e, 256 * vc + ec:256 * vc + 256:2]
 
         rs = keep.tile([P, 16], F32, name="rs")
-        colp = bank(7, "colp")
-        for w in range(4):
+        live = {}
+
+        def rowsum(w):
             nc.vector.tensor_reduce(out=rs[:, w:w + 1], in_=a_sb[:, w, 0, :], axis=AX.X, op=ALU.add)
-            nc.scalar.activation(out=junk[:], in_=a_sb[:, w, 1, :], func=ACT.Copy,
+            nc.scalar.activation(out=junk[:, w, :], in_=a_sb[:, w, 1, :], func=ACT.Copy,
                                  accum_out=rs[:, 8 + w:9 + w])
+
+        def colsum(w):
+            if w == 0:
+                live["colp"] = bank(7, "colp")
+            colp = live["colp"]
             for e in range(2):
                 for v in range(4):
                     i0 = ((w * 2 + e) * 4 + v) * 2
@@ -100,15 +114,11 @@ def tile_selfexpression2_kernel(tc, x, Coefficient2, A, out):
                         nc.tensor.matmul(colp[:, i0:i0 + 2], lhsT=a_cols(w, ew, v, e), rhs=ones_b[:],
                                          start=(ew == 0), stop=(ew == 1))
 
-        tiles = [(0, 0, 0), (0, 1, 0), (1, 0, 0), (1, 1, 0), (2, 0, 2), (2, 1, 0), (3, 0, 2), (3, 1, 0),
-                 (4, 1, 0), (5, 1, 0), (6, 1, 2), (7, 1, 2)]
-        s2p = {}
-
         def add_tile(n):
-            a, G, t0 = tiles[n]
+            a, G, t0 = TILES[n]
             v, e = a // 2, a % 2
-            tl = bank(n % 4, "s2p")
-            s2p[n] = tl
+            tl = bank(S2_BANKS[n % len(S2_BANKS)], "s2p")
+            live["s2p", n] = tl
             for t2 in range(t0, 4):
                 c = 4 * G + t2
                 vc, ec = c // 2, c % 2
@@ -118,176 +128,238 @@ def tile_selfexpression2_kernel(tc, x, Coefficient2, A, out):
                 if c == a:
                     nc.tensor.matmul(o, lhsT=ident_b[:], rhs=two_eye[:], start=False, stop=True)
 
-        for n in range(4):
-            add_tile(n)
-
         c_gw = c_g[:].bitcast(F32)
-        for ib in range(8):
-            ctp = bank(5 + ib % 2, "ctp")
+
+        def c_tr(ib, b):
+            ctp = bank(b, "ctp")
+            live["ctp", ib] = ctp
             for vv in range(4):
                 nc.tensor.transpose(
                     ctp[:, 128 * vv:128 * (vv + 1)],
                     c_sb[:, ib, :].bitcast(F32)[:, 128 * vv:128 * (vv + 1)],
                     ident_f[:])
-            nc.scalar.copy(out=c_gw[:, :, 128 * ib:128 * (ib + 1), :],
-                           in_=ctp[:].rearrange("p (g u i) -> p g i u", g=2, u=2))
+
+        def c_ev(ib, eng):
+            eng(out=c_gw[:, :, 128 * ib:128 * (ib + 1), :],
+                in_=live["ctp", ib][:].rearrange("p (g u i) -> p g i u", g=2, u=2))
 
         def small(name):
             return keep.tile([P, 8], F32, name=name)
 
-        cs = small("cs")
-        nc.vector.tensor_reduce(
-            out=cs[:], in_=colp[:, 0:64].rearrange("p (w a n) -> p a n w", w=4, n=2)[:, :, 0, :],
-            axis=AX.X, op=ALU.add)
-        d = small("d")
-        nc.vector.scalar_tensor_tensor(
-            out=d[:].rearrange("p (e v) -> p e v", e=2),
-            in0=rs[:].rearrange("p (e c) -> p e c", e=2)[:, :, 0:4], scalar=2.0,
-            in1=cs[:].rearrange("p (e v) -> p e v", e=2), op0=ALU.add, op1=ALU.add)
-        dm = small("dm")
-        nc.vector.tensor_scalar_max(out=dm[:], in0=d[:], scalar1=TINY)
-        mask = small("mask")
-        nc.vector.tensor_single_scalar(out=mask[:], in_=d[:], scalar=0.0, op=ALU.is_gt)
-        rt = small("rt")
-        nc.scalar.activation(out=rt[:], in_=dm[:], func=ACT.Sqrt)
-        y0 = small("y0")
-        nc.vector.reciprocal(out=y0[:], in_=rt[:])
-        t1 = small("t1")
-        nc.vector.tensor_mul(out=t1[:], in0=dm[:], in1=y0[:])
-        t2_ = small("t2_")
-        nc.vector.scalar_tensor_tensor(out=t2_[:], in0=t1[:], scalar=-0.5, in1=y0[:], op0=ALU.mult, op1=ALU.mult)
-        y1 = small("y1")
-        nc.vector.scalar_tensor_tensor(out=y1[:], in0=t2_[:], scalar=1.5, in1=y0[:], op0=ALU.add, op1=ALU.mult)
-        t3 = small("t3")
-        nc.vector.tensor_mul(out=t3[:], in0=dm[:], in1=y1[:])
-        y1m = small("y1m")
-        nc.vector.tensor_mul(out=y1m[:], in0=y1[:], in1=mask[:])
-        t4 = small("t4")
-        nc.vector.scalar_tensor_tensor(out=t4[:], in0=t3[:], scalar=-0.5, in1=y1[:], op0=ALU.mult, op1=ALU.mult)
-        dinv = small("dinv")
-        nc.vector.scalar_tensor_tensor(out=dinv[:], in0=t4[:], scalar=1.5, in1=y1m[:], op0=ALU.add, op1=ALU.mult)
+        cs, d, dm, mask, rt, y0 = small("cs"), small("d"), small("dm"), small("mask"), small("rt"), small("y0")
+        t1, t2s, y1, t3, y1m, t4, dinv = (small("t1"), small("t2s"), small("y1"), small("t3"), small("y1m"),
+                                          small("t4"), small("dinv"))
+
+        def chain_a():
+            nc.vector.tensor_reduce(
+                out=cs[:], in_=live["colp"][:, 0:64].rearrange("p (w a n) -> p a n w", w=4, n=2)[:, :, 0, :],
+                axis=AX.X, op=ALU.add)
+            nc.vector.scalar_tensor_tensor(
+                out=d[:].rearrange("p (e v) -> p e v", e=2),
+                in0=rs[:].rearrange("p (e c) -> p e c", e=2)[:, :, 0:4], scalar=2.0,
+                in1=cs[:].rearrange("p (e v) -> p e v", e=2), op0=ALU.add, op1=ALU.add)
+            nc.vector.tensor_scalar_max(out=dm[:], in0=d[:], scalar1=TINY)
+            nc.scalar.activation(out=rt[:], in_=dm[:], func=ACT.Sqrt)
+            nc.vector.tensor_single_scalar(out=mask[:], in_=d[:], scalar=0.0, op=ALU.is_gt)
+
+        def chain_b():
+            stt = nc.vector.scalar_tensor_tensor
+            nc.vector.reciprocal(out=y0[:], in_=rt[:])
+            nc.vector.tensor_mul(out=t1[:], in0=dm[:], in1=y0[:])
+            stt(out=t2s[:], in0=t1[:], scalar=-0.5, in1=y0[:], op0=ALU.mult, op1=ALU.mult)
+            stt(out=y1[:], in0=t2s[:], scalar=1.5, in1=y0[:], op0=ALU.add, op1=ALU.mult)
+            nc.vector.tensor_mul(out=t3[:], in0=dm[:], in1=y1[:])
+            nc.vector.tensor_mul(out=y1m[:], in0=y1[:], in1=mask[:])
+            stt(out=t4[:], in0=t3[:], scalar=-0.5, in1=y1[:], op0=ALU.mult, op1=ALU.mult)
+            stt(out=dinv[:], in0=t4[:], scalar=1.5, in1=y1m[:], op0=ALU.add, op1=ALU.mult)
 
         def dcol(a):
             i = 4 * (a % 2) + a // 2
             return dinv[:, i:i + 1]
 
-        rowp = [bank(7, "rowp0"), bank(4, "rowp1")]
-        for a in range(8):
-            nc.tensor.transpose(rowp[a // 4][:, 128 * (a % 4):128 * (a % 4 + 1)],
-                                dcol(a).to_broadcast([P, P]), ident_f[:])
-        nc.vector.tensor_copy(out=dj_sb[:, 0:512], in_=rowp[0][:])
-        nc.scalar.copy(out=dj_sb[:, 512:1024], in_=rowp[1][:])
-
-        for g in range(2):
-            for h in range(2):
-                quantise(c_g, c_c, c_s, g, 512 * h, 512)
+        def bcast():
+            rowp = [bank(7, "rowp0"), bank(ROW1_BANK, "rowp1")]
+            for a in range(8):
+                nc.tensor.transpose(rowp[a // 4][:, 128 * (a % 4):128 * (a % 4 + 1)],
+                                    dcol(a).to_broadcast([P, P]), ident_f[:])
+            V(out=dj_sb[:, 0:512], in_=rowp[0][:])
+            S(out=dj_sb[:, 512:1024], in_=rowp[1][:])
 
         def scale_tile(n):
-            a, G, t0 = tiles[n]
+            a, G, t0 = TILES[n]
             lo, hi = 512 * G + 128 * t0, 512 * (G + 1)
             nc.vector.scalar_tensor_tensor(
-                out=adjn[:, a, lo:hi], in0=s2p[n][:, 128 * t0:512], scalar=dcol(a),
+                out=adjn[:, a, lo:hi], in0=live["s2p", n][:, 128 * t0:512], scalar=dcol(a),
                 in1=dj_sb[:, lo:hi], op0=ALU.mult, op1=ALU.mult)
 
-        def lower_diag(g, b):
+        def ld_tr(g, b):
             ld = bank_bf(b, "ld")
+            live["ld", g] = ld
             for r in range(2):
                 a = 4 * g + 2 + r
                 for cc in range(2):
                     c = 4 * g + cc
                     q = 2 * r + cc
                     nc.tensor.transpose(ld[:, 128 * q:128 * (q + 1)], adjn[:, c, 128 * a:128 * (a + 1)], ident_b[:])
-            nc.scalar.copy(out=adjn[:, 4 * g + 2:4 * g + 4, 512 * g:512 * g + 256],
-                           in_=ld[:, 0:512].rearrange("p (r j) -> p r j", r=2))
 
-        def lower_off(h, b):
+        def ld_ev(g, eng):
+            eng(out=adjn[:, 4 * g + 2:4 * g + 4, 512 * g:512 * g + 256],
+                in_=live["ld", g][:, 0:512].rearrange("p (r j) -> p r j", r=2))
+
+        def lt_tr(h, b):
             lt = bank_bf(b, "lt")
+            live["lt", h] = lt
             for cl in range(2):
                 c = 2 * h + cl
                 for t in range(4):
                     q = 4 * cl + t
                     nc.tensor.transpose(lt[:, 128 * q:128 * (q + 1)], adjn[:, c, 128 * (4 + t):128 * (5 + t)],
                                         ident_b[:])
-            nc.scalar.copy(out=adj_g[:, 1, 256 * h:256 * (h + 1), :].rearrange("p (cl j) t -> p cl j t", cl=2),
-                           in_=lt[:].rearrange("p (cl t j) -> p cl j t", cl=2, t=4))
 
-        for n in range(4):
-            scale_tile(n)
+        def lt_ev(h, eng):
+            eng(out=adj_g[:, 1, 256 * h:256 * (h + 1), :].rearrange("p (cl j) t -> p cl j t", cl=2),
+                in_=live["lt", h][:].rearrange("p (cl t j) -> p cl j t", cl=2, t=4))
+
+        def rg_adj(g, c0, cols, eng):
+            regroup(eng, adj_g[:, g, c0:c0 + cols, :], adjn[:, 4 * g:4 * g + 4, c0:c0 + cols])
+
+        def q_adj(g, c0, cols):
+            quantise(adj_g, adj_c, adj_s, g, c0, cols)
+
+        def m1(G, ib, b, t_lo, t_hi):
+            if t_lo == 0:
+                live["yp", G, ib] = bank(b, "yp")
+            yp = live["yp", G, ib]
+            for t2 in range(t_lo, t_hi):
+                j0 = 512 * G + 128 * t2
+                for g in range(2):
+                    nc.tensor.matmul_mx(
+                        out=yp[:, 128 * t2:128 * (t2 + 1)],
+                        lhsT=adj_c[:, g, j0:j0 + 128].bitcast(FP8X4),
+                        lhsT_scale=adj_s[:, g, j0:j0 + 128],
+                        rhs=c_c[:, g, 128 * ib:128 * (ib + 1)].bitcast(FP8X4),
+                        rhs_scale=c_s[:, g, 128 * ib:128 * (ib + 1)],
+                        start=(g == 0), stop=(g == 1))
+
+        def y_ev(G, ib, eng):
+            eng(out=y_g[:, G, 128 * ib:128 * (ib + 1), :],
+                in_=live["yp", G, ib][:].rearrange("p (t i) -> p i t", t=4))
+
+        def x_rg(G, c0, cols, eng):
+            regroup(eng, x_g[:, G, c0:c0 + cols, :], x_sb[:, G, :, c0:c0 + cols])
+
+        def m2(ib, h, b):
+            op = bank(b, "op")
+            live["op", ib, h] = op
+            for G in range(2):
+                nc.tensor.matmul_mx(
+                    out=op[:],
+                    lhsT=y_c[:, G, 128 * ib:128 * (ib + 1)].bitcast(FP8X4),
+                    lhsT_scale=y_s[:, G, 128 * ib:128 * (ib + 1)],
+                    rhs=x_c[:, G, 512 * h:512 * (h + 1)].bitcast(FP8X4),
+                    rhs_scale=x_s[:, G, 512 * h:512 * (h + 1)],
+                    start=(G == 0), stop=(G == 1))
+
+        def o_ev(ib, h, eng):
+            ost = stage.tile([P, 512], F32, name="ost")
+            eng(out=ost[:], in_=live["op", ib, h][:])
+            nc.sync.dma_start(out=out[128 * ib:128 * (ib + 1), 512 * h:512 * (h + 1)], in_=ost[:])
+
+        for w in range(4):
+            colsum(w)
+            rowsum(w)
+        chain_a()
+        c_tr(0, 5)
+        c_tr(1, 6)
+        c_ev(0, S)
+        c_ev(1, S)
+        add_tile(0)
+        add_tile(1)
+        c_tr(2, 5)
+        c_ev(2, S)
+        add_tile(2)
+        chain_b()
+        quantise(c_g, c_c, c_s, 0, 0, 256)
+        quantise(c_g, c_c, c_s, 1, 0, 256)
+        bcast()
+        c_tr(3, 6)
+        c_ev(3, S)
+        x_rg(0, 0, 256, S)
+        add_tile(3)
+        scale_tile(0)
+        scale_tile(1)
         add_tile(4)
+        scale_tile(2)
         add_tile(5)
-        lower_diag(0, 5)
-        lower_off(0, 6)
+        scale_tile(3)
+        ld_tr(0, 4)
+        lt_tr(0, 7)
+        ld_ev(0, S)
+        lt_ev(0, S)
+        x_rg(0, 256, 256, S)
         add_tile(6)
         add_tile(7)
-        for n in range(4, 8):
-            scale_tile(n)
-        lower_off(1, 5)
-        for n in range(8, 12):
-            add_tile(n)
-        regroup(nc.vector.tensor_copy, adj_g[:, 0, 0:512, :], adjn[:, 0:4, 0:512])
-        quantise(adj_g, adj_c, adj_s, 0, 0, 512)
-        quantise(adj_g, adj_c, adj_s, 1, 0, 512)
-        regroup(nc.scalar.copy, adj_g[:, 0, 512:1024, :], adjn[:, 0:4, 512:1024])
-        for n in range(8, 12):
-            scale_tile(n)
-        lower_diag(1, 0)
-        regroup(nc.vector.tensor_copy, adj_g[:, 1, 512:1024, :], adjn[:, 4:8, 512:1024])
-        quantise(adj_g, adj_c, adj_s, 0, 512, 512)
-        quantise(adj_g, adj_c, adj_s, 1, 512, 512)
-
-        nb = [0]
-
-        def next_bank(name, banks):
-            b = banks[nb[0] % len(banks)]
-            nb[0] += 1
-            return bank(b, name)
-
-        def first_matmul(G, banks, engines):
-            for ib in range(8):
-                yp = next_bank("yp", banks)
-                for t2 in range(4):
-                    j0 = 512 * G + 128 * t2
-                    for g in range(2):
-                        nc.tensor.matmul_mx(
-                            out=yp[:, 128 * t2:128 * (t2 + 1)],
-                            lhsT=adj_c[:, g, j0:j0 + 128].bitcast(FP8X4),
-                            lhsT_scale=adj_s[:, g, j0:j0 + 128],
-                            rhs=c_c[:, g, 128 * ib:128 * (ib + 1)].bitcast(FP8X4),
-                            rhs_scale=c_s[:, g, 128 * ib:128 * (ib + 1)],
-                            start=(g == 0), stop=(g == 1))
-                engines[ib % len(engines)](
-                    out=y_g[:, G, 128 * ib:128 * (ib + 1), :],
-                    in_=yp[:].rearrange("p (t i) -> p i t", t=4))
-                if ib % 2 == 1:
-                    quantise(y_g, y_c, y_s, G, 128 * (ib - 1), 256)
-
-        first_matmul(0, [4, 5, 6, 7], [nc.scalar.copy])
-
-        for G in range(2):
-            regroup(nc.vector.tensor_copy, x_g[:, G, 0:512, :], x_sb[:, G, :, 0:512])
-            regroup(nc.scalar.copy, x_g[:, G, 512:1024, :], x_sb[:, G, :, 512:1024])
-        for G in range(2):
-            for h in range(2):
-                quantise(x_g, x_c, x_s, G, 512 * h, 512)
-
-        all_banks = [0, 1, 2, 3, 4, 5, 6, 7]
-        nb[0] = 0
-        first_matmul(1, all_banks, [nc.scalar.copy, nc.vector.tensor_copy])
-
+        scale_tile(4)
+        scale_tile(5)
+        scale_tile(6)
+        scale_tile(7)
+        add_tile(8)
+        lt_tr(1, 4)
+        lt_ev(1, S)
+        c_tr(4, 5)
+        c_tr(5, 6)
+        c_ev(4, S)
+        c_ev(5, S)
+        rg_adj(0, 0, 512, V)
+        quantise(c_g, c_c, c_s, 0, 256, 256)
+        q_adj(0, 0, 512)
+        quantise(c_g, c_c, c_s, 1, 256, 256)
+        q_adj(1, 0, 512)
+        c_tr(6, 5)
+        c_tr(7, 6)
+        c_ev(6, S)
+        c_ev(7, S)
+        scale_tile(8)
+        quantise(c_g, c_c, c_s, 0, 512, 512)
+        quantise(c_g, c_c, c_s, 1, 512, 512)
+        YB0 = [4, 7, 5, 6]
         for ib in range(8):
-            ost = stage.tile([P, N], F32, name="ost")
-            for h in range(2):
-                op = next_bank("op", all_banks)
-                for G in range(2):
-                    nc.tensor.matmul_mx(
-                        out=op[:],
-                        lhsT=y_c[:, G, 128 * ib:128 * (ib + 1)].bitcast(FP8X4),
-                        lhsT_scale=y_s[:, G, 128 * ib:128 * (ib + 1)],
-                        rhs=x_c[:, G, 512 * h:512 * (h + 1)].bitcast(FP8X4),
-                        rhs_scale=x_s[:, G, 512 * h:512 * (h + 1)],
-                        start=(G == 0), stop=(G == 1))
-                if h == 0:
-                    nc.vector.tensor_copy(out=ost[:, 0:512], in_=op[:])
-                else:
-                    nc.scalar.copy(out=ost[:, 512:1024], in_=op[:])
-            nc.sync.dma_start(out=out[128 * ib:128 * (ib + 1), :], in_=ost[:])
+            m1(0, ib, YB0[ib % 4], 0, 4)
+            y_ev(0, ib, S)
+            if ib < 3:
+                add_tile(9 + ib)
+                scale_tile(9 + ib)
+            if ib == 0:
+                rg_adj(0, 512, 512, V)
+            if ib == 2:
+                rg_adj(1, 512, 512, V)
+                q_adj(0, 512, 512)
+                q_adj(1, 512, 512)
+            if ib in (2, 5):
+                x_rg(1, 256 * (ib // 4), 256, S)
+            if ib == 3:
+                quantise(y_g, y_c, y_s, 0, 0, 512)
+                x_rg(0, 512, 512, V)
+            if ib == 7:
+                quantise(y_g, y_c, y_s, 0, 512, 512)
+        quantise(x_g, x_c, x_s, 0, 0, 512)
+        quantise(x_g, x_c, x_s, 1, 0, 512)
+        B = [0, 1, 2, 3, 4, 5, 6, 7]
+        k = 0
+        for ib in range(8):
+            m1(1, ib, B[k % 8], 0, 4)
+            k += 1
+            y_ev(1, ib, S)
+            if ib % 2 == 1:
+                quantise(y_g, y_c, y_s, 1, 128 * (ib - 1), 256)
+            if ib == 1:
+                x_rg(1, 512, 512, V)
+            if ib == 3:
+                quantise(x_g, x_c, x_s, 0, 512, 512)
+            if ib == 5:
+                quantise(x_g, x_c, x_s, 1, 512, 512)
+        for h in range(2):
+            for ib in range(8):
+                m2(ib, h, B[k % 8])
+                k += 1
+                o_ev(ib, h, V if ib % 2 == 0 else S)

@@ -13,14 +13,13 @@ ACT = mybir.ActivationFunctionType
 AX = mybir.AxisListType
 
 OST_BUFS = 16
-S2_BANKS = [0, 1, 2, 3]
-ROW1_BANK = 4
+ROW1_BANK = 5
 P = 128
 N = 1024
 FLOPS = 2 * 2 * N * N * N
 TINY = 2.0 ** -100
-TILES = [(0, 0, 0), (0, 1, 0), (1, 0, 0), (1, 1, 0), (2, 0, 2), (2, 1, 0), (3, 0, 2), (3, 1, 0),
-         (4, 1, 0), (5, 1, 0), (6, 1, 0), (7, 1, 0)]
+TILES = [(0, 0, 0, 0, 0), (0, 1, 0, 1, 0), (1, 0, 0, 2, 0), (1, 1, 0, 3, 0), (2, 0, 2, 4, 256), (2, 1, 0, 0, 0),
+         (3, 0, 2, 4, 0), (3, 1, 0, 1, 0), (4, 1, 0, 2, 0), (5, 1, 0, 3, 0), (6, 1, 0, 4, 0), (7, 1, 0, 0, 0)]
 
 
 def tile_selfexpression2_kernel(tc, x, Coefficient2, A, out):
@@ -55,13 +54,19 @@ def tile_selfexpression2_kernel(tc, x, Coefficient2, A, out):
             nc.sync.dma_start(out=a_sb[:, v, :, :],
                               in_=A[256 * v:256 * (v + 1), :].rearrange("(p e) c -> p e c", e=2))
         c_sb = keep.tile([P, 8, N], BF16, name="c_sb")
+        x_sb = keep.tile([P, 2, 4, N], BF16, name="x_sb")
+
+        def load_x(v):
+            nc.sync.dma_start(out=x_sb[:, v // 2, 2 * (v % 2):2 * (v % 2) + 2, :],
+                              in_=x[256 * v:256 * (v + 1), :].rearrange("(p e) d -> p e d", e=2))
+
+        load_x(0)
+        load_x(1)
         for h in range(4):
             nc.sync.dma_start(out=c_sb[:, 2 * h:2 * h + 2, :],
                               in_=Coefficient2[256 * h:256 * (h + 1), :].rearrange("(b p) k -> p b k", p=P))
-        x_sb = keep.tile([P, 2, 4, N], BF16, name="x_sb")
-        for v in range(4):
-            nc.sync.dma_start(out=x_sb[:, v // 2, 2 * (v % 2):2 * (v % 2) + 2, :],
-                              in_=x[256 * v:256 * (v + 1), :].rearrange("(p e) d -> p e d", e=2))
+        load_x(2)
+        load_x(3)
 
         adjn = keep.tile([P, 8, N], BF16, name="adjn")
         dj_sb = keep.tile([P, N], F32, name="dj_sb")
@@ -103,30 +108,52 @@ def tile_selfexpression2_kernel(tc, x, Coefficient2, A, out):
             nc.scalar.activation(out=junk[:, w, :], in_=a_sb[:, w, 1, :], func=ACT.Copy,
                                  accum_out=rs[:, 8 + w:9 + w])
 
-        def colsum(w):
-            if w == 0:
+        def colsum_group(w, i):
+            if w == 0 and i == 0:
                 live["colp"] = bank(7, "colp")
             colp = live["colp"]
-            for e in range(2):
-                for v in range(4):
-                    i0 = ((w * 2 + e) * 4 + v) * 2
-                    for ew in range(2):
-                        nc.tensor.matmul(colp[:, i0:i0 + 2], lhsT=a_cols(w, ew, v, e), rhs=ones_b[:],
-                                         start=(ew == 0), stop=(ew == 1))
+            i0 = (w * 8 + i) * 2
+            e, v = i // 4, i % 4
+            for ew in range(2):
+                nc.tensor.matmul(colp[:, i0:i0 + 2], lhsT=a_cols(w, ew, v, e), rhs=ones_b[:],
+                                 start=(ew == 0), stop=(ew == 1))
 
-        def add_tile(n):
-            a, G, t0 = TILES[n]
+        def colsum(w, blocks):
+            for i in range(8):
+                colsum_group(w, i)
+                if i % 2 == 1 and i // 2 < len(blocks):
+                    n, t2 = blocks[i // 2]
+                    add_blocks(n, t2, t2 + 1)
+
+        def add_blocks(n, t_lo, t_hi):
+            a, G, t0, b, col0 = TILES[n]
             v, e = a // 2, a % 2
-            tl = bank(S2_BANKS[n % len(S2_BANKS)], "s2p")
-            live["s2p", n] = tl
-            for t2 in range(t0, 4):
+            if t_lo == t0:
+                live["s2p", n] = live["s2p", 4] if n == 6 else bank(b, "s2p")
+            tl = live["s2p", n]
+            for t2 in range(t_lo, t_hi):
                 c = 4 * G + t2
                 vc, ec = c // 2, c % 2
-                o = tl[:, 128 * t2:128 * (t2 + 1)]
+                o = tl[:, col0 + 128 * (t2 - t0):col0 + 128 * (t2 - t0 + 1)]
                 nc.tensor.matmul(o, lhsT=ident_b[:], rhs=a_cols(v, e, vc, ec), start=True, stop=False)
                 nc.tensor.matmul(o, lhsT=a_cols(vc, ec, v, e), rhs=ident_b[:], start=False, stop=(c != a))
                 if c == a:
                     nc.tensor.matmul(o, lhsT=ident_b[:], rhs=two_eye[:], start=False, stop=True)
+
+        def add_tile(n):
+            add_blocks(n, TILES[n][2], 4)
+
+        wb = keep.tile([P, 512], BF16, name="wb", align_bytes=64)
+        wz = keep.tile([P, P], U32, name="wz", align_bytes=64)
+        sz = keep.tile([P, P], U8, name="sz", align_bytes=64)
+        nc.vector.memset(wb[:], 1.0)
+        nc.vector.quantize_mx(out=wz[:].bitcast(FP8X4), scales=sz[:], in_=wb[:])
+
+        def spin(count, b):
+            dummy = bank(b, "dummy")
+            for i in range(count):
+                nc.tensor.matmul_mx(out=dummy[:, 0:P], lhsT=wz[:].bitcast(FP8X4), lhsT_scale=sz[:],
+                                    rhs=wz[:].bitcast(FP8X4), rhs_scale=sz[:], start=True, stop=True)
 
         c_gw = c_g[:].bitcast(F32)
 
@@ -186,10 +213,10 @@ def tile_selfexpression2_kernel(tc, x, Coefficient2, A, out):
             S(out=dj_sb[:, 512:1024], in_=rowp[1][:])
 
         def scale_tile(n):
-            a, G, t0 = TILES[n]
+            a, G, t0, b, col0 = TILES[n]
             lo, hi = 512 * G + 128 * t0, 512 * (G + 1)
             nc.vector.scalar_tensor_tensor(
-                out=adjn[:, a, lo:hi], in0=live["s2p", n][:, 128 * t0:512], scalar=dcol(a),
+                out=adjn[:, a, lo:hi], in0=live["s2p", n][:, col0:col0 + hi - lo], scalar=dcol(a),
                 in1=dj_sb[:, lo:hi], op0=ALU.mult, op1=ALU.mult)
 
         def ld_tr(g, b):
@@ -265,86 +292,93 @@ def tile_selfexpression2_kernel(tc, x, Coefficient2, A, out):
             eng(out=ost[:], in_=live["op", ib, h][:])
             nc.sync.dma_start(out=out[128 * ib:128 * (ib + 1), 512 * h:512 * (h + 1)], in_=ost[:])
 
-        for w in range(4):
-            colsum(w)
-            rowsum(w)
+        spin(24, 3)
+        colsum(0, [(0, 0), (0, 1), (2, 0), (2, 1)])
+        rowsum(0)
+        colsum(1, [(0, 2), (0, 3), (2, 2), (2, 3)])
+        rowsum(1)
+        colsum(2, [(1, 0), (1, 1), (3, 0), (3, 1)])
+        rowsum(2)
+        colsum(3, [(1, 2)])
+        rowsum(3)
+        x_rg(0, 0, 512, V)
+        x_rg(0, 512, 256, S)
         chain_a()
+        x_rg(0, 768, 256, S)
+        add_blocks(1, 3, 4)
         c_tr(0, 5)
-        c_tr(1, 6)
         c_ev(0, S)
+        add_blocks(3, 2, 4)
+        c_tr(1, 6)
         c_ev(1, S)
-        add_tile(0)
-        add_tile(1)
-        c_tr(2, 5)
-        c_ev(2, S)
-        add_tile(2)
-        chain_b()
-        quantise(c_g, c_c, c_s, 0, 0, 256)
-        quantise(c_g, c_c, c_s, 1, 0, 256)
-        bcast()
-        c_tr(3, 6)
-        c_ev(3, S)
-        x_rg(0, 0, 256, S)
-        add_tile(3)
-        scale_tile(0)
-        scale_tile(1)
+        spin(8, 7)
         add_tile(4)
-        scale_tile(2)
+        chain_b()
+        bcast()
+        add_blocks(6, 2, 3)
+        c_tr(2, 6)
+        c_ev(2, S)
+        add_blocks(6, 3, 4)
+        scale_tile(0)
+        c_tr(3, 7)
+        c_ev(3, S)
+        scale_tile(1)
         add_tile(5)
+        c_tr(4, 5)
+        c_ev(4, S)
+        scale_tile(2)
+        add_tile(7)
+        c_tr(5, 6)
+        c_ev(5, S)
         scale_tile(3)
-        ld_tr(0, 4)
-        lt_tr(0, 7)
+        add_tile(8)
+        ld_tr(0, 7)
+        lt_tr(0, 5)
         ld_ev(0, S)
         lt_ev(0, S)
-        x_rg(0, 256, 256, S)
-        add_tile(6)
-        add_tile(7)
         scale_tile(4)
         scale_tile(5)
+        add_tile(9)
+        c_tr(6, 6)
+        c_ev(6, S)
         scale_tile(6)
         scale_tile(7)
-        add_tile(8)
-        lt_tr(1, 4)
+        lt_tr(1, 7)
         lt_ev(1, S)
-        c_tr(4, 5)
-        c_tr(5, 6)
-        c_ev(4, S)
-        c_ev(5, S)
-        rg_adj(0, 0, 512, V)
-        quantise(c_g, c_c, c_s, 0, 256, 256)
-        q_adj(0, 0, 512)
-        quantise(c_g, c_c, c_s, 1, 256, 256)
-        q_adj(1, 0, 512)
-        c_tr(6, 5)
-        c_tr(7, 6)
-        c_ev(6, S)
+        add_tile(10)
+        c_tr(7, 5)
         c_ev(7, S)
+        add_tile(11)
+        rg_adj(0, 0, 512, V)
+        quantise(c_g, c_c, c_s, 0, 0, 512)
+        q_adj(0, 0, 512)
+        quantise(c_g, c_c, c_s, 1, 0, 512)
+        q_adj(1, 0, 512)
         scale_tile(8)
+        scale_tile(9)
         quantise(c_g, c_c, c_s, 0, 512, 512)
         quantise(c_g, c_c, c_s, 1, 512, 512)
-        YB0 = [4, 7, 5, 6]
+        scale_tile(10)
+        scale_tile(11)
+        rg_adj(1, 512, 512, V)
+        YB0 = [6, 7, 5, 1, 2, 3, 4, 0]
         for ib in range(8):
-            m1(0, ib, YB0[ib % 4], 0, 4)
+            m1(0, ib, YB0[ib], 0, 4)
             y_ev(0, ib, S)
-            if ib < 3:
-                add_tile(9 + ib)
-                scale_tile(9 + ib)
-            if ib == 0:
-                rg_adj(0, 512, 512, V)
+            if ib in (0, 2):
+                rg_adj(0, 512 + 128 * ib, 256, S)
             if ib == 2:
-                rg_adj(1, 512, 512, V)
-                q_adj(0, 512, 512)
                 q_adj(1, 512, 512)
-            if ib in (2, 5):
-                x_rg(1, 256 * (ib // 4), 256, S)
+                q_adj(0, 512, 512)
+                x_rg(1, 0, 512, V)
             if ib == 3:
                 quantise(y_g, y_c, y_s, 0, 0, 512)
-                x_rg(0, 512, 512, V)
+                quantise(x_g, x_c, x_s, 0, 0, 512)
+                quantise(x_g, x_c, x_s, 1, 0, 512)
             if ib == 7:
                 quantise(y_g, y_c, y_s, 0, 512, 512)
-        quantise(x_g, x_c, x_s, 0, 0, 512)
-        quantise(x_g, x_c, x_s, 1, 0, 512)
-        B = [0, 1, 2, 3, 4, 5, 6, 7]
+                x_rg(1, 512, 512, V)
+        B = [6, 7, 5, 1, 2, 3, 4, 0]
         k = 0
         for ib in range(8):
             m1(1, ib, B[k % 8], 0, 4)
@@ -352,12 +386,8 @@ def tile_selfexpression2_kernel(tc, x, Coefficient2, A, out):
             y_ev(1, ib, S)
             if ib % 2 == 1:
                 quantise(y_g, y_c, y_s, 1, 128 * (ib - 1), 256)
-            if ib == 1:
-                x_rg(1, 512, 512, V)
-            if ib == 3:
-                quantise(x_g, x_c, x_s, 0, 512, 512)
-            if ib == 5:
-                quantise(x_g, x_c, x_s, 1, 512, 512)
+            if ib in (1, 3):
+                quantise(x_g, x_c, x_s, ib // 2, 512, 512)
         for h in range(2):
             for ib in range(8):
                 m2(ib, h, B[k % 8])

@@ -13,13 +13,12 @@ ACT = mybir.ActivationFunctionType
 AX = mybir.AxisListType
 
 OST_BUFS = 16
-ROW1_BANK = 5
 P = 128
 N = 1024
 FLOPS = 2 * 2 * N * N * N
 TINY = 2.0 ** -100
 TILES = [(0, 0, 0, 0, 0), (0, 1, 0, 1, 0), (1, 0, 0, 2, 0), (1, 1, 0, 3, 0), (2, 0, 2, 4, 256), (2, 1, 0, 0, 0),
-         (3, 0, 2, 4, 0), (3, 1, 0, 1, 0), (4, 1, 0, 2, 0), (5, 1, 0, 3, 0), (6, 1, 0, 4, 0), (7, 1, 0, 0, 0)]
+         (3, 0, 2, 4, 0), (3, 1, 0, 2, 0), (4, 1, 0, 4, 0), (5, 1, 0, 1, 0), (6, 1, 0, 3, 0), (7, 1, 0, 0, 0)]
 
 
 def tile_selfexpression2_kernel(tc, x, Coefficient2, A, out):
@@ -60,13 +59,11 @@ def tile_selfexpression2_kernel(tc, x, Coefficient2, A, out):
             nc.sync.dma_start(out=x_sb[:, v // 2, 2 * (v % 2):2 * (v % 2) + 2, :],
                               in_=x[256 * v:256 * (v + 1), :].rearrange("(p e) d -> p e d", e=2))
 
-        load_x(0)
-        load_x(1)
         for h in range(4):
             nc.sync.dma_start(out=c_sb[:, 2 * h:2 * h + 2, :],
                               in_=Coefficient2[256 * h:256 * (h + 1), :].rearrange("(b p) k -> p b k", p=P))
-        load_x(2)
-        load_x(3)
+        for v in range(4):
+            load_x(v)
 
         adjn = keep.tile([P, 8, N], BF16, name="adjn")
         dj_sb = keep.tile([P, N], F32, name="dj_sb")
@@ -204,13 +201,11 @@ def tile_selfexpression2_kernel(tc, x, Coefficient2, A, out):
             i = 4 * (a % 2) + a // 2
             return dinv[:, i:i + 1]
 
-        def bcast():
-            rowp = [bank(7, "rowp0"), bank(ROW1_BANK, "rowp1")]
-            for a in range(8):
-                nc.tensor.transpose(rowp[a // 4][:, 128 * (a % 4):128 * (a % 4 + 1)],
-                                    dcol(a).to_broadcast([P, P]), ident_f[:])
-            V(out=dj_sb[:, 0:512], in_=rowp[0][:])
-            S(out=dj_sb[:, 512:1024], in_=rowp[1][:])
+        def bcast(g, b, eng):
+            rowp = bank(b, "rowp")
+            for t in range(4):
+                nc.tensor.transpose(rowp[:, 128 * t:128 * (t + 1)], dcol(4 * g + t).to_broadcast([P, P]), ident_f[:])
+            eng(out=dj_sb[:, 512 * g:512 * (g + 1)], in_=rowp[:])
 
         def scale_tile(n):
             a, G, t0, b, col0 = TILES[n]
@@ -293,66 +288,61 @@ def tile_selfexpression2_kernel(tc, x, Coefficient2, A, out):
             nc.sync.dma_start(out=out[128 * ib:128 * (ib + 1), 512 * h:512 * (h + 1)], in_=ost[:])
 
         spin(24, 3)
-        colsum(0, [(0, 0), (0, 1), (2, 0), (2, 1)])
-        rowsum(0)
-        colsum(1, [(0, 2), (0, 3), (2, 2), (2, 3)])
-        rowsum(1)
-        colsum(2, [(1, 0), (1, 1), (3, 0), (3, 1)])
-        rowsum(2)
-        colsum(3, [(1, 2)])
-        rowsum(3)
-        x_rg(0, 0, 512, V)
-        x_rg(0, 512, 256, S)
+        for w in range(4):
+            colsum(w, [])
+            rowsum(w)
         chain_a()
-        x_rg(0, 768, 256, S)
-        add_blocks(1, 3, 4)
         c_tr(0, 5)
         c_ev(0, S)
-        add_blocks(3, 2, 4)
+        add_tile(0)
         c_tr(1, 6)
         c_ev(1, S)
-        spin(8, 7)
+        add_tile(2)
+        c_tr(2, 5)
+        c_ev(2, S)
+        c_tr(3, 6)
+        c_ev(3, S)
         add_tile(4)
         chain_b()
-        bcast()
-        add_blocks(6, 2, 3)
-        c_tr(2, 6)
-        c_ev(2, S)
-        add_blocks(6, 3, 4)
+        quantise(c_g, c_c, c_s, 0, 0, 256)
+        quantise(c_g, c_c, c_s, 1, 0, 256)
+        bcast(0, 7, V)
+        add_tile(6)
+        add_tile(1)
+        bcast(1, 7, S)
+        add_tile(3)
         scale_tile(0)
-        c_tr(3, 7)
-        c_ev(3, S)
-        scale_tile(1)
-        add_tile(5)
-        c_tr(4, 5)
-        c_ev(4, S)
         scale_tile(2)
-        add_tile(7)
-        c_tr(5, 6)
-        c_ev(5, S)
-        scale_tile(3)
-        add_tile(8)
-        ld_tr(0, 7)
-        lt_tr(0, 5)
+        add_tile(5)
+        ld_tr(0, 5)
         ld_ev(0, S)
-        lt_ev(0, S)
         scale_tile(4)
-        scale_tile(5)
-        add_tile(9)
-        c_tr(6, 6)
-        c_ev(6, S)
         scale_tile(6)
+        add_tile(7)
+        c_tr(4, 6)
+        c_ev(4, S)
+        scale_tile(1)
+        scale_tile(3)
+        lt_tr(0, 7)
+        lt_ev(0, S)
+        add_tile(8)
+        c_tr(5, 5)
+        c_ev(5, S)
+        scale_tile(5)
         scale_tile(7)
-        lt_tr(1, 7)
+        lt_tr(1, 6)
         lt_ev(1, S)
+        add_tile(9)
+        c_tr(6, 5)
+        c_ev(6, S)
         add_tile(10)
-        c_tr(7, 5)
+        c_tr(7, 7)
         c_ev(7, S)
         add_tile(11)
         rg_adj(0, 0, 512, V)
-        quantise(c_g, c_c, c_s, 0, 0, 512)
+        quantise(c_g, c_c, c_s, 0, 256, 256)
         q_adj(0, 0, 512)
-        quantise(c_g, c_c, c_s, 1, 0, 512)
+        quantise(c_g, c_c, c_s, 1, 256, 256)
         q_adj(1, 0, 512)
         scale_tile(8)
         scale_tile(9)
@@ -361,7 +351,7 @@ def tile_selfexpression2_kernel(tc, x, Coefficient2, A, out):
         scale_tile(10)
         scale_tile(11)
         rg_adj(1, 512, 512, V)
-        YB0 = [6, 7, 5, 1, 2, 3, 4, 0]
+        YB0 = [6, 7, 5, 2, 4, 1, 3, 0]
         for ib in range(8):
             m1(0, ib, YB0[ib], 0, 4)
             y_ev(0, ib, S)
@@ -370,26 +360,25 @@ def tile_selfexpression2_kernel(tc, x, Coefficient2, A, out):
             if ib == 2:
                 q_adj(1, 512, 512)
                 q_adj(0, 512, 512)
+                x_rg(0, 0, 512, V)
                 x_rg(1, 0, 512, V)
-            if ib == 3:
-                quantise(y_g, y_c, y_s, 0, 0, 512)
                 quantise(x_g, x_c, x_s, 0, 0, 512)
                 quantise(x_g, x_c, x_s, 1, 0, 512)
-            if ib == 7:
-                quantise(y_g, y_c, y_s, 0, 512, 512)
-                x_rg(1, 512, 512, V)
-        B = [6, 7, 5, 1, 2, 3, 4, 0]
-        k = 0
+        quantise(y_g, y_c, y_s, 0, 0, 512)
+        quantise(y_g, y_c, y_s, 0, 512, 512)
         for ib in range(8):
-            m1(1, ib, B[k % 8], 0, 4)
-            k += 1
+            m1(1, ib, YB0[ib], 0, 4)
             y_ev(1, ib, S)
             if ib % 2 == 1:
                 quantise(y_g, y_c, y_s, 1, 128 * (ib - 1), 256)
-            if ib in (1, 3):
-                quantise(x_g, x_c, x_s, ib // 2, 512, 512)
-        for h in range(2):
-            for ib in range(8):
-                m2(ib, h, B[k % 8])
-                k += 1
-                o_ev(ib, h, V if ib % 2 == 0 else S)
+            if ib == 5:
+                x_rg(0, 512, 512, V)
+        x_rg(1, 512, 512, V)
+        quantise(x_g, x_c, x_s, 0, 512, 512)
+        quantise(x_g, x_c, x_s, 1, 512, 512)
+        for ib in range(8):
+            m2(ib, 0, YB0[ib])
+            o_ev(ib, 0, S)
+        for ib in range(8):
+            m2(ib, 1, YB0[ib])
+            o_ev(ib, 1, V if ib % 2 == 0 else S)

@@ -12,13 +12,14 @@ ALU = mybir.AluOpType
 ACT = mybir.ActivationFunctionType
 AX = mybir.AxisListType
 
-OST_BUFS = 16
+OST_BUFS = 17
 P = 128
 N = 1024
 FLOPS = 2 * 2 * N * N * N
 TINY = 2.0 ** -100
-TILES = [(0, 0, 0, 0, 0), (0, 1, 0, 1, 0), (1, 0, 0, 2, 0), (1, 1, 0, 3, 0), (2, 0, 2, 4, 256), (2, 1, 0, 0, 0),
-         (3, 0, 2, 4, 0), (3, 1, 0, 2, 0), (4, 1, 0, 4, 0), (5, 1, 0, 1, 0), (6, 1, 0, 3, 0), (7, 1, 0, 0, 0)]
+TILES = [(0, 0, 0, 0, 0), (0, 1, 0, 3, 0), (1, 0, 0, 2, 0), (1, 1, 0, 0, 0), (2, 0, 2, 4, 256), (2, 1, 0, 2, 0),
+         (3, 0, 2, 4, 0), (3, 1, 0, 4, 0), (4, 1, 0, 3, 0), (5, 1, 0, 0, 0), (6, 1, 2, 2, 256), (7, 1, 2, 2, 0)]
+SHARES = {6: 4, 11: 10}
 
 
 def tile_selfexpression2_kernel(tc, x, Coefficient2, A, out):
@@ -67,6 +68,7 @@ def tile_selfexpression2_kernel(tc, x, Coefficient2, A, out):
 
         adjn = keep.tile([P, 8, N], BF16, name="adjn")
         dj_sb = keep.tile([P, N], F32, name="dj_sb")
+        s2_sb = keep.tile([P, 4, 512], F32, name="s2_sb")
         junk = keep.tile([P, 4, N], BF16, name="junk")
         adj_g = keep.tile([P, 2, N, 4], BF16, name="adj_g", align_bytes=64)
         c_g = keep.tile([P, 2, N, 4], BF16, name="c_g", align_bytes=64)
@@ -126,7 +128,7 @@ def tile_selfexpression2_kernel(tc, x, Coefficient2, A, out):
             a, G, t0, b, col0 = TILES[n]
             v, e = a // 2, a % 2
             if t_lo == t0:
-                live["s2p", n] = live["s2p", 4] if n == 6 else bank(b, "s2p")
+                live["s2p", n] = live["s2p", SHARES[n]] if n in SHARES else bank(b, "s2p")
             tl = live["s2p", n]
             for t2 in range(t_lo, t_hi):
                 c = 4 * G + t2
@@ -171,8 +173,7 @@ def tile_selfexpression2_kernel(tc, x, Coefficient2, A, out):
             return keep.tile([P, 8], F32, name=name)
 
         cs, d, dm, mask, rt, y0 = small("cs"), small("d"), small("dm"), small("mask"), small("rt"), small("y0")
-        t1, t2s, y1, t3, y1m, t4, dinv = (small("t1"), small("t2s"), small("y1"), small("t3"), small("y1m"),
-                                          small("t4"), small("dinv"))
+        t1, t2s, y0m, dinv = small("t1"), small("t2s"), small("y0m"), small("dinv")
 
         def chain_a():
             nc.vector.tensor_reduce(
@@ -190,22 +191,29 @@ def tile_selfexpression2_kernel(tc, x, Coefficient2, A, out):
             stt = nc.vector.scalar_tensor_tensor
             nc.vector.reciprocal(out=y0[:], in_=rt[:])
             nc.vector.tensor_mul(out=t1[:], in0=dm[:], in1=y0[:])
+            nc.vector.tensor_mul(out=y0m[:], in0=y0[:], in1=mask[:])
             stt(out=t2s[:], in0=t1[:], scalar=-0.5, in1=y0[:], op0=ALU.mult, op1=ALU.mult)
-            stt(out=y1[:], in0=t2s[:], scalar=1.5, in1=y0[:], op0=ALU.add, op1=ALU.mult)
-            nc.vector.tensor_mul(out=t3[:], in0=dm[:], in1=y1[:])
-            nc.vector.tensor_mul(out=y1m[:], in0=y1[:], in1=mask[:])
-            stt(out=t4[:], in0=t3[:], scalar=-0.5, in1=y1[:], op0=ALU.mult, op1=ALU.mult)
-            stt(out=dinv[:], in0=t4[:], scalar=1.5, in1=y1m[:], op0=ALU.add, op1=ALU.mult)
+            stt(out=dinv[:], in0=t2s[:], scalar=1.5, in1=y0m[:], op0=ALU.add, op1=ALU.mult)
 
         def dcol(a):
             i = 4 * (a % 2) + a // 2
             return dinv[:, i:i + 1]
 
-        def bcast(g, b, eng):
+        def bcast(g, b):
             rowp = bank(b, "rowp")
+            live["rowp", g] = rowp
             for t in range(4):
                 nc.tensor.transpose(rowp[:, 128 * t:128 * (t + 1)], dcol(4 * g + t).to_broadcast([P, P]), ident_f[:])
-            eng(out=dj_sb[:, 512 * g:512 * (g + 1)], in_=rowp[:])
+
+        def s2_ev(n, eng):
+            a, G, t0, b, col0 = TILES[n]
+            eng(out=s2_sb[:, a, 128 * t0:512], in_=live["s2p", n][:, col0:col0 + 512 - 128 * t0])
+
+        def scale_sb(n):
+            a, G, t0, b, col0 = TILES[n]
+            nc.vector.scalar_tensor_tensor(
+                out=adjn[:, a, 128 * t0:512], in0=s2_sb[:, a, 128 * t0:512], scalar=dcol(a),
+                in1=live["rowp", 0][:, 128 * t0:512], op0=ALU.mult, op1=ALU.mult)
 
         def scale_tile(n):
             a, G, t0, b, col0 = TILES[n]
@@ -282,10 +290,10 @@ def tile_selfexpression2_kernel(tc, x, Coefficient2, A, out):
                     rhs_scale=x_s[:, G, 512 * h:512 * (h + 1)],
                     start=(G == 0), stop=(G == 1))
 
-        def o_ev(ib, h, eng):
-            ost = stage.tile([P, 512], F32, name="ost")
-            eng(out=ost[:], in_=live["op", ib, h][:])
-            nc.sync.dma_start(out=out[128 * ib:128 * (ib + 1), 512 * h:512 * (h + 1)], in_=ost[:])
+        def o_ev(ib, h, eng, c0=0, cols=512):
+            ost = stage.tile([P, cols], F32, name="ost")
+            eng(out=ost[:], in_=live["op", ib, h][:, c0:c0 + cols])
+            nc.sync.dma_start(out=out[128 * ib:128 * (ib + 1), 512 * h + c0:512 * h + c0 + cols], in_=ost[:])
 
         spin(24, 3)
         for w in range(4):
@@ -293,52 +301,59 @@ def tile_selfexpression2_kernel(tc, x, Coefficient2, A, out):
             rowsum(w)
         chain_a()
         c_tr(0, 5)
-        c_ev(0, S)
-        add_tile(0)
         c_tr(1, 6)
+        c_ev(0, S)
         c_ev(1, S)
+        add_tile(0)
+        s2_ev(0, S)
         add_tile(2)
-        c_tr(2, 5)
-        c_ev(2, S)
-        c_tr(3, 6)
-        c_ev(3, S)
+        s2_ev(2, S)
         add_tile(4)
+        add_tile(6)
+        s2_ev(4, S)
+        s2_ev(6, S)
         chain_b()
         quantise(c_g, c_c, c_s, 0, 0, 256)
         quantise(c_g, c_c, c_s, 1, 0, 256)
-        bcast(0, 7, V)
-        add_tile(6)
+        bcast(0, 7)
+        bcast(1, 1)
+        S(out=dj_sb[:, 512:1024], in_=live["rowp", 1][:])
+        c_tr(2, 5)
+        c_tr(3, 6)
+        c_ev(2, S)
+        c_ev(3, S)
+        scale_sb(0)
         add_tile(1)
-        bcast(1, 7, S)
+        scale_sb(2)
         add_tile(3)
-        scale_tile(0)
-        scale_tile(2)
-        add_tile(5)
-        ld_tr(0, 5)
+        ld_tr(0, 1)
         ld_ev(0, S)
-        scale_tile(4)
-        scale_tile(6)
+        x_rg(0, 0, 256, S)
+        scale_sb(4)
+        add_tile(5)
+        scale_sb(6)
         add_tile(7)
-        c_tr(4, 6)
-        c_ev(4, S)
         scale_tile(1)
         scale_tile(3)
         lt_tr(0, 7)
         lt_ev(0, S)
-        add_tile(8)
-        c_tr(5, 5)
-        c_ev(5, S)
+        c_tr(4, 5)
+        c_tr(5, 6)
         scale_tile(5)
         scale_tile(7)
-        lt_tr(1, 6)
+        lt_tr(1, 1)
         lt_ev(1, S)
-        add_tile(9)
-        c_tr(6, 5)
-        c_ev(6, S)
-        add_tile(10)
+        c_tr(6, 4)
+        add_tile(8)
         c_tr(7, 7)
-        c_ev(7, S)
+        add_tile(9)
+        add_tile(10)
         add_tile(11)
+        c_ev(4, S)
+        c_ev(5, S)
+        c_ev(6, S)
+        c_ev(7, S)
+        rg_adj(0, 512, 256, S)
         rg_adj(0, 0, 512, V)
         quantise(c_g, c_c, c_s, 0, 256, 256)
         q_adj(0, 0, 512)
@@ -346,39 +361,51 @@ def tile_selfexpression2_kernel(tc, x, Coefficient2, A, out):
         q_adj(1, 0, 512)
         scale_tile(8)
         scale_tile(9)
-        quantise(c_g, c_c, c_s, 0, 512, 512)
-        quantise(c_g, c_c, c_s, 1, 512, 512)
         scale_tile(10)
         scale_tile(11)
-        rg_adj(1, 512, 512, V)
-        YB0 = [6, 7, 5, 2, 4, 1, 3, 0]
+        quantise(c_g, c_c, c_s, 0, 512, 512)
+        quantise(c_g, c_c, c_s, 1, 512, 512)
+        YB0 = [1, 5, 6, 4, 7, 3, 0, 2]
         for ib in range(8):
             m1(0, ib, YB0[ib], 0, 4)
-            y_ev(0, ib, S)
-            if ib in (0, 2):
-                rg_adj(0, 512 + 128 * ib, 256, S)
-            if ib == 2:
+            if ib == 1:
+                ld_tr(1, 3)
+                ld_ev(1, S)
+                rg_adj(0, 768, 256, S)
+                rg_adj(1, 512, 512, V)
                 q_adj(1, 512, 512)
                 q_adj(0, 512, 512)
-                x_rg(0, 0, 512, V)
+                x_rg(0, 256, 256, V)
                 x_rg(1, 0, 512, V)
                 quantise(x_g, x_c, x_s, 0, 0, 512)
                 quantise(x_g, x_c, x_s, 1, 0, 512)
-        quantise(y_g, y_c, y_s, 0, 0, 512)
-        quantise(y_g, y_c, y_s, 0, 512, 512)
+            if ib >= 2:
+                y_ev(0, ib - 2, S)
+            if ib == 5:
+                quantise(y_g, y_c, y_s, 0, 0, 512)
+                x_rg(0, 512, 256, V)
+        y_ev(0, 6, S)
+        y_ev(0, 7, S)
         for ib in range(8):
             m1(1, ib, YB0[ib], 0, 4)
             y_ev(1, ib, S)
             if ib % 2 == 1:
                 quantise(y_g, y_c, y_s, 1, 128 * (ib - 1), 256)
+            if ib == 1:
+                quantise(y_g, y_c, y_s, 0, 512, 512)
+            if ib == 3:
+                x_rg(0, 768, 256, V)
             if ib == 5:
-                x_rg(0, 512, 512, V)
-        x_rg(1, 512, 512, V)
+                x_rg(1, 512, 256, V)
+        x_rg(1, 768, 256, V)
         quantise(x_g, x_c, x_s, 0, 512, 512)
         quantise(x_g, x_c, x_s, 1, 512, 512)
         for ib in range(8):
             m2(ib, 0, YB0[ib])
             o_ev(ib, 0, S)
-        for ib in range(8):
+        for ib in range(7):
             m2(ib, 1, YB0[ib])
             o_ev(ib, 1, V if ib % 2 == 0 else S)
+        m2(7, 1, YB0[7])
+        o_ev(7, 1, V, 0, 256)
+        o_ev(7, 1, S, 256, 256)

@@ -18,8 +18,8 @@ N = 1024
 FLOPS = 2 * 2 * N * N * N
 TINY = 2.0 ** -100
 TILES = [(0, 0, 0, 0, 0), (0, 1, 0, 3, 0), (1, 0, 0, 2, 0), (1, 1, 0, 0, 0), (2, 0, 2, 4, 256), (2, 1, 0, 2, 0),
-         (3, 0, 2, 4, 0), (3, 1, 0, 4, 0), (4, 1, 0, 3, 0), (5, 1, 0, 0, 0), (6, 1, 2, 2, 256), (7, 1, 2, 2, 0)]
-SHARES = {6: 4, 11: 10}
+         (3, 0, 2, 4, 0), (3, 1, 0, 4, 0), (4, 1, 0, 3, 0), (5, 1, 0, 0, 0), (6, 1, 0, 2, 0), (7, 1, 0, 5, 0)]
+SHARES = {6: 4}
 
 
 def tile_selfexpression2_kernel(tc, x, Coefficient2, A, out):
@@ -348,7 +348,6 @@ def tile_selfexpression2_kernel(tc, x, Coefficient2, A, out):
         c_tr(7, 7)
         add_tile(9)
         add_tile(10)
-        add_tile(11)
         c_ev(4, S)
         c_ev(5, S)
         c_ev(6, S)
@@ -362,15 +361,15 @@ def tile_selfexpression2_kernel(tc, x, Coefficient2, A, out):
         scale_tile(8)
         scale_tile(9)
         scale_tile(10)
-        scale_tile(11)
         quantise(c_g, c_c, c_s, 0, 512, 512)
         quantise(c_g, c_c, c_s, 1, 512, 512)
-        YB0 = [1, 5, 6, 4, 7, 3, 0, 2]
+        YB0 = [1, 6, 4, 7, 3, 0, 2, 5]
         for ib in range(8):
             m1(0, ib, YB0[ib], 0, 4)
+            if ib == 0:
+                add_tile(11)
+                scale_tile(11)
             if ib == 1:
-                ld_tr(1, 3)
-                ld_ev(1, S)
                 rg_adj(0, 768, 256, S)
                 rg_adj(1, 512, 512, V)
                 q_adj(1, 512, 512)

@@ -12,14 +12,13 @@ ALU = mybir.AluOpType
 ACT = mybir.ActivationFunctionType
 AX = mybir.AxisListType
 
-OST_BUFS = 17
+OST_BUFS = 16
 P = 128
 N = 1024
 FLOPS = 2 * 2 * N * N * N
 TINY = 2.0 ** -100
-TILES = [(0, 0, 0, 0, 0), (0, 1, 0, 3, 0), (1, 0, 0, 2, 0), (1, 1, 0, 0, 0), (2, 0, 2, 4, 256), (2, 1, 0, 2, 0),
-         (3, 0, 2, 4, 0), (3, 1, 0, 4, 0), (4, 1, 0, 3, 0), (5, 1, 0, 0, 0), (6, 1, 0, 2, 0), (7, 1, 0, 5, 0)]
-SHARES = {6: 4}
+TILES = [(0, 0, 0, 0, 0), (0, 1, 0, 1, 0), (1, 0, 0, 2, 0), (1, 1, 0, 3, 0), (2, 0, 2, 4, 256), (2, 1, 0, 0, 0),
+         (3, 0, 2, 4, 0), (3, 1, 0, 2, 0), (4, 1, 0, 4, 0), (5, 1, 0, 1, 0), (6, 1, 0, 3, 0), (7, 1, 0, 0, 0)]
 
 
 def tile_selfexpression2_kernel(tc, x, Coefficient2, A, out):
@@ -68,7 +67,6 @@ def tile_selfexpression2_kernel(tc, x, Coefficient2, A, out):
 
         adjn = keep.tile([P, 8, N], BF16, name="adjn")
         dj_sb = keep.tile([P, N], F32, name="dj_sb")
-        s2_sb = keep.tile([P, 4, 512], F32, name="s2_sb")
         junk = keep.tile([P, 4, N], BF16, name="junk")
         adj_g = keep.tile([P, 2, N, 4], BF16, name="adj_g", align_bytes=64)
         c_g = keep.tile([P, 2, N, 4], BF16, name="c_g", align_bytes=64)
@@ -128,7 +126,7 @@ def tile_selfexpression2_kernel(tc, x, Coefficient2, A, out):
             a, G, t0, b, col0 = TILES[n]
             v, e = a // 2, a % 2
             if t_lo == t0:
-                live["s2p", n] = live["s2p", SHARES[n]] if n in SHARES else bank(b, "s2p")
+                live["s2p", n] = live["s2p", 4] if n == 6 else bank(b, "s2p")
             tl = live["s2p", n]
             for t2 in range(t_lo, t_hi):
                 c = 4 * G + t2
@@ -173,7 +171,8 @@ def tile_selfexpression2_kernel(tc, x, Coefficient2, A, out):
             return keep.tile([P, 8], F32, name=name)
 
         cs, d, dm, mask, rt, y0 = small("cs"), small("d"), small("dm"), small("mask"), small("rt"), small("y0")
-        t1, t2s, y0m, dinv = small("t1"), small("t2s"), small("y0m"), small("dinv")
+        t1, t2s, y1, t3, y1m, t4, dinv = (small("t1"), small("t2s"), small("y1"), small("t3"), small("y1m"),
+                                          small("t4"), small("dinv"))
 
         def chain_a():
             nc.vector.tensor_reduce(
@@ -191,29 +190,22 @@ def tile_selfexpression2_kernel(tc, x, Coefficient2, A, out):
             stt = nc.vector.scalar_tensor_tensor
             nc.vector.reciprocal(out=y0[:], in_=rt[:])
             nc.vector.tensor_mul(out=t1[:], in0=dm[:], in1=y0[:])
-            nc.vector.tensor_mul(out=y0m[:], in0=y0[:], in1=mask[:])
             stt(out=t2s[:], in0=t1[:], scalar=-0.5, in1=y0[:], op0=ALU.mult, op1=ALU.mult)
-            stt(out=dinv[:], in0=t2s[:], scalar=1.5, in1=y0m[:], op0=ALU.add, op1=ALU.mult)
+            stt(out=y1[:], in0=t2s[:], scalar=1.5, in1=y0[:], op0=ALU.add, op1=ALU.mult)
+            nc.vector.tensor_mul(out=t3[:], in0=dm[:], in1=y1[:])
+            nc.vector.tensor_mul(out=y1m[:], in0=y1[:], in1=mask[:])
+            stt(out=t4[:], in0=t3[:], scalar=-0.5, in1=y1[:], op0=ALU.mult, op1=ALU.mult)
+            stt(out=dinv[:], in0=t4[:], scalar=1.5, in1=y1m[:], op0=ALU.add, op1=ALU.mult)
 
         def dcol(a):
             i = 4 * (a % 2) + a // 2
             return dinv[:, i:i + 1]
 
-        def bcast(g, b):
+        def bcast(g, b, eng):
             rowp = bank(b, "rowp")
-            live["rowp", g] = rowp
             for t in range(4):
                 nc.tensor.transpose(rowp[:, 128 * t:128 * (t + 1)], dcol(4 * g + t).to_broadcast([P, P]), ident_f[:])
-
-        def s2_ev(n, eng):
-            a, G, t0, b, col0 = TILES[n]
-            eng(out=s2_sb[:, a, 128 * t0:512], in_=live["s2p", n][:, col0:col0 + 512 - 128 * t0])
-
-        def scale_sb(n):
-            a, G, t0, b, col0 = TILES[n]
-            nc.vector.scalar_tensor_tensor(
-                out=adjn[:, a, 128 * t0:512], in0=s2_sb[:, a, 128 * t0:512], scalar=dcol(a),
-                in1=live["rowp", 0][:, 128 * t0:512], op0=ALU.mult, op1=ALU.mult)
+            eng(out=dj_sb[:, 512 * g:512 * (g + 1)], in_=rowp[:])
 
         def scale_tile(n):
             a, G, t0, b, col0 = TILES[n]
@@ -278,6 +270,11 @@ def tile_selfexpression2_kernel(tc, x, Coefficient2, A, out):
         def x_rg(G, c0, cols, eng):
             regroup(eng, x_g[:, G, c0:c0 + cols, :], x_sb[:, G, :, c0:c0 + cols])
 
+        def x_rg_pool(G, c0, cols):
+            nc.gpsimd.tensor_scalar(out=x_g[:, G, c0:c0 + cols, :],
+                                    in0=x_sb[:, G, :, c0:c0 + cols].rearrange("p t j -> p j t"),
+                                    scalar1=1.0, scalar2=0.0, op0=ALU.mult, op1=ALU.add)
+
         def m2(ib, h, b):
             op = bank(b, "op")
             live["op", ib, h] = op
@@ -290,10 +287,10 @@ def tile_selfexpression2_kernel(tc, x, Coefficient2, A, out):
                     rhs_scale=x_s[:, G, 512 * h:512 * (h + 1)],
                     start=(G == 0), stop=(G == 1))
 
-        def o_ev(ib, h, eng, c0=0, cols=512):
-            ost = stage.tile([P, cols], F32, name="ost")
-            eng(out=ost[:], in_=live["op", ib, h][:, c0:c0 + cols])
-            nc.sync.dma_start(out=out[128 * ib:128 * (ib + 1), 512 * h + c0:512 * h + c0 + cols], in_=ost[:])
+        def o_ev(ib, h, eng):
+            ost = stage.tile([P, 512], F32, name="ost")
+            eng(out=ost[:], in_=live["op", ib, h][:])
+            nc.sync.dma_start(out=out[128 * ib:128 * (ib + 1), 512 * h:512 * (h + 1)], in_=ost[:])
 
         spin(24, 3)
         for w in range(4):
@@ -301,58 +298,54 @@ def tile_selfexpression2_kernel(tc, x, Coefficient2, A, out):
             rowsum(w)
         chain_a()
         c_tr(0, 5)
-        c_tr(1, 6)
         c_ev(0, S)
-        c_ev(1, S)
         add_tile(0)
-        s2_ev(0, S)
+        c_tr(1, 6)
+        c_ev(1, S)
         add_tile(2)
-        s2_ev(2, S)
+        c_tr(2, 5)
+        c_ev(2, S)
+        c_tr(3, 6)
+        c_ev(3, S)
         add_tile(4)
-        add_tile(6)
-        s2_ev(4, S)
-        s2_ev(6, S)
         chain_b()
         quantise(c_g, c_c, c_s, 0, 0, 256)
         quantise(c_g, c_c, c_s, 1, 0, 256)
-        bcast(0, 7)
-        bcast(1, 1)
-        S(out=dj_sb[:, 512:1024], in_=live["rowp", 1][:])
-        c_tr(2, 5)
-        c_tr(3, 6)
-        c_ev(2, S)
-        c_ev(3, S)
-        scale_sb(0)
+        bcast(0, 7, V)
+        x_rg_pool(0, 0, 512)
+        x_rg_pool(0, 512, 256)
+        add_tile(6)
         add_tile(1)
-        scale_sb(2)
+        bcast(1, 7, S)
         add_tile(3)
-        ld_tr(0, 1)
-        ld_ev(0, S)
-        x_rg(0, 0, 256, S)
-        scale_sb(4)
+        scale_tile(0)
+        scale_tile(2)
         add_tile(5)
-        scale_sb(6)
+        ld_tr(0, 5)
+        ld_ev(0, S)
+        scale_tile(4)
+        scale_tile(6)
         add_tile(7)
+        c_tr(4, 6)
+        c_ev(4, S)
         scale_tile(1)
         scale_tile(3)
         lt_tr(0, 7)
         lt_ev(0, S)
-        c_tr(4, 5)
-        c_tr(5, 6)
+        add_tile(8)
+        c_tr(5, 5)
+        c_ev(5, S)
         scale_tile(5)
         scale_tile(7)
-        lt_tr(1, 1)
+        lt_tr(1, 6)
         lt_ev(1, S)
-        c_tr(6, 4)
-        add_tile(8)
-        c_tr(7, 7)
         add_tile(9)
-        add_tile(10)
-        c_ev(4, S)
-        c_ev(5, S)
+        c_tr(6, 5)
         c_ev(6, S)
+        add_tile(10)
+        c_tr(7, 7)
         c_ev(7, S)
-        rg_adj(0, 512, 256, S)
+        add_tile(11)
         rg_adj(0, 0, 512, V)
         quantise(c_g, c_c, c_s, 0, 256, 256)
         q_adj(0, 0, 512)
@@ -360,51 +353,38 @@ def tile_selfexpression2_kernel(tc, x, Coefficient2, A, out):
         q_adj(1, 0, 512)
         scale_tile(8)
         scale_tile(9)
-        scale_tile(10)
         quantise(c_g, c_c, c_s, 0, 512, 512)
         quantise(c_g, c_c, c_s, 1, 512, 512)
-        YB0 = [1, 6, 4, 7, 3, 0, 2, 5]
+        scale_tile(10)
+        scale_tile(11)
+        rg_adj(1, 512, 512, V)
+        YB0 = [6, 7, 5, 2, 4, 1, 3, 0]
         for ib in range(8):
             m1(0, ib, YB0[ib], 0, 4)
-            if ib == 0:
-                add_tile(11)
-                scale_tile(11)
-            if ib == 1:
-                rg_adj(0, 768, 256, S)
-                rg_adj(1, 512, 512, V)
+            y_ev(0, ib, S)
+            if ib in (0, 2):
+                rg_adj(0, 512 + 128 * ib, 256, S)
+            if ib == 2:
                 q_adj(1, 512, 512)
                 q_adj(0, 512, 512)
-                x_rg(0, 256, 256, V)
                 x_rg(1, 0, 512, V)
                 quantise(x_g, x_c, x_s, 0, 0, 512)
                 quantise(x_g, x_c, x_s, 1, 0, 512)
-            if ib >= 2:
-                y_ev(0, ib - 2, S)
-            if ib == 5:
-                quantise(y_g, y_c, y_s, 0, 0, 512)
-                x_rg(0, 512, 256, V)
-        y_ev(0, 6, S)
-        y_ev(0, 7, S)
+        quantise(y_g, y_c, y_s, 0, 0, 512)
+        quantise(y_g, y_c, y_s, 0, 512, 512)
         for ib in range(8):
             m1(1, ib, YB0[ib], 0, 4)
             y_ev(1, ib, S)
             if ib % 2 == 1:
                 quantise(y_g, y_c, y_s, 1, 128 * (ib - 1), 256)
-            if ib == 1:
-                quantise(y_g, y_c, y_s, 0, 512, 512)
-            if ib == 3:
-                x_rg(0, 768, 256, V)
             if ib == 5:
-                x_rg(1, 512, 256, V)
-        x_rg(1, 768, 256, V)
+                x_rg(0, 768, 256, V)
+        x_rg(1, 512, 512, V)
         quantise(x_g, x_c, x_s, 0, 512, 512)
         quantise(x_g, x_c, x_s, 1, 512, 512)
         for ib in range(8):
             m2(ib, 0, YB0[ib])
             o_ev(ib, 0, S)
-        for ib in range(7):
+        for ib in range(8):
             m2(ib, 1, YB0[ib])
             o_ev(ib, 1, V if ib % 2 == 0 else S)
-        m2(7, 1, YB0[7])
-        o_ev(7, 1, V, 0, 256)
-        o_ev(7, 1, S, 256, 256)

@@ -140,18 +140,6 @@ def tile_selfexpression2_kernel(tc, x, Coefficient2, A, out):
         def add_tile(n):
             add_blocks(n, TILES[n][2], 4)
 
-        wb = keep.tile([P, 512], BF16, name="wb", align_bytes=64)
-        wz = keep.tile([P, P], U32, name="wz", align_bytes=64)
-        sz = keep.tile([P, P], U8, name="sz", align_bytes=64)
-        nc.vector.memset(wb[:], 1.0)
-        nc.vector.quantize_mx(out=wz[:].bitcast(FP8X4), scales=sz[:], in_=wb[:])
-
-        def spin(count, b):
-            dummy = bank(b, "dummy")
-            for i in range(count):
-                nc.tensor.matmul_mx(out=dummy[:, 0:P], lhsT=wz[:].bitcast(FP8X4), lhsT_scale=sz[:],
-                                    rhs=wz[:].bitcast(FP8X4), rhs_scale=sz[:], start=True, stop=True)
-
         c_gw = c_g[:].bitcast(F32)
 
         def c_tr(ib, b):
@@ -270,11 +258,6 @@ def tile_selfexpression2_kernel(tc, x, Coefficient2, A, out):
         def x_rg(G, c0, cols, eng):
             regroup(eng, x_g[:, G, c0:c0 + cols, :], x_sb[:, G, :, c0:c0 + cols])
 
-        def x_rg_pool(G, c0, cols):
-            nc.gpsimd.tensor_scalar(out=x_g[:, G, c0:c0 + cols, :],
-                                    in0=x_sb[:, G, :, c0:c0 + cols].rearrange("p t j -> p j t"),
-                                    scalar1=1.0, scalar2=0.0, op0=ALU.mult, op1=ALU.add)
-
         def m2(ib, h, b):
             op = bank(b, "op")
             live["op", ib, h] = op
@@ -292,7 +275,6 @@ def tile_selfexpression2_kernel(tc, x, Coefficient2, A, out):
             eng(out=ost[:], in_=live["op", ib, h][:])
             nc.sync.dma_start(out=out[128 * ib:128 * (ib + 1), 512 * h:512 * (h + 1)], in_=ost[:])
 
-        spin(24, 3)
         for w in range(4):
             colsum(w, [])
             rowsum(w)
@@ -312,8 +294,6 @@ def tile_selfexpression2_kernel(tc, x, Coefficient2, A, out):
         quantise(c_g, c_c, c_s, 0, 0, 256)
         quantise(c_g, c_c, c_s, 1, 0, 256)
         bcast(0, 7, V)
-        x_rg_pool(0, 0, 512)
-        x_rg_pool(0, 512, 256)
         add_tile(6)
         add_tile(1)
         bcast(1, 7, S)
@@ -367,6 +347,7 @@ def tile_selfexpression2_kernel(tc, x, Coefficient2, A, out):
             if ib == 2:
                 q_adj(1, 512, 512)
                 q_adj(0, 512, 512)
+                x_rg(0, 0, 512, V)
                 x_rg(1, 0, 512, V)
                 quantise(x_g, x_c, x_s, 0, 0, 512)
                 quantise(x_g, x_c, x_s, 1, 0, 512)
@@ -378,7 +359,7 @@ def tile_selfexpression2_kernel(tc, x, Coefficient2, A, out):
             if ib % 2 == 1:
                 quantise(y_g, y_c, y_s, 1, 128 * (ib - 1), 256)
             if ib == 5:
-                x_rg(0, 768, 256, V)
+                x_rg(0, 512, 512, V)
         x_rg(1, 512, 512, V)
         quantise(x_g, x_c, x_s, 0, 512, 512)
         quantise(x_g, x_c, x_s, 1, 512, 512)

from contextlib import ExitStack

import concourse.mybir as mybir
from concourse.masks import make_identity

F32 = mybir.dt.float32
BF16 = mybir.dt.bfloat16
U32 = mybir.dt.uint32
U8 = mybir.dt.uint8
FP8X4 = mybir.dt.float8_e4m3fn_x4
ALU = mybir.AluOpType
ACT = mybir.ActivationFunctionType
AX = mybir.AxisListType

OST_BUFS = 16
P = 128
N = 1024
FLOPS = 2 * 2 * N * N * N
TINY = 2.0 ** -100
TILES = [(0, 0, 0, 0, 0), (0, 1, 0, 1, 0), (1, 0, 0, 2, 0), (1, 1, 0, 3, 0), (2, 0, 2, 4, 256), (2, 1, 0, 0, 0),
         (3, 0, 2, 4, 0), (3, 1, 0, 2, 0), (4, 1, 0, 4, 0), (5, 1, 0, 1, 0), (6, 1, 0, 3, 0), (7, 1, 0, 0, 0)]


def tile_selfexpression2_kernel(tc, x, Coefficient2, A, out):
    nc = tc.nc
    with ExitStack() as ctx:
        keep = ctx.enter_context(tc.tile_pool(name="keep", bufs=1))
        stage = ctx.enter_context(tc.tile_pool(name="stage", bufs=OST_BUFS))
        psum = ctx.enter_context(tc.psum_pool(name="psum", bufs=1))
        ctx.enter_context(tc.manual_schedule())

        def bank(i, name):
            return psum.tile([P, 512], F32, tag="bank%d" % i, name=name)

        def bank_bf(i, name):
            return psum.tile([P, 1024], BF16, tag="bank%d" % i, name=name)

        ident_f = keep.tile([P, P], F32, name="ident_f")
        ident_b = keep.tile([P, P], BF16, name="ident_b")
        make_identity(nc, ident_b[:])
        make_identity(nc, ident_f[:])
        two_eye = keep.tile([P, P], BF16, name="two_eye")
        nc.gpsimd.tensor_scalar(out=two_eye[:], in0=ident_f[:], scalar1=2.0, scalar2=0.0,
                                op0=ALU.mult, op1=ALU.add)
        ones_b = keep.tile([P, 2], BF16, name="ones_b")
        nc.vector.memset(ones_b[:], 1.0)
        warm = keep.tile([P, 1], F32, name="warm")
        nc.vector.memset(warm[:], 1.0)
        nc.scalar.activation(out=warm[:], in_=warm[:], func=ACT.Sqrt)

        a_sb = keep.tile([P, 4, 2, N], BF16, name="a_sb")
        for v in range(4):
            nc.sync.dma_start(out=a_sb[:, v, :, :],
                              in_=A[256 * v:256 * (v + 1), :].rearrange("(p e) c -> p e c", e=2))
        c_sb = keep.tile([P, 8, N], BF16, name="c_sb")
        x_sb = keep.tile([P, 2, 4, N], BF16, name="x_sb")

        def load_x(v):
            nc.sync.dma_start(out=x_sb[:, v // 2, 2 * (v % 2):2 * (v % 2) + 2, :],
                              in_=x[256 * v:256 * (v + 1), :].rearrange("(p e) d -> p e d", e=2))

        for h in range(4):
            nc.sync.dma_start(out=c_sb[:, 2 * h:2 * h + 2, :],
                              in_=Coefficient2[256 * h:256 * (h + 1), :].rearrange("(b p) k -> p b k", p=P))
        for v in range(4):
            load_x(v)

        adjn = keep.tile([P, 8, N], BF16, name="adjn")
        dj_sb = keep.tile([P, N], F32, name="dj_sb")
        junk = keep.tile([P, 4, N], BF16, name="junk")
        adj_g = keep.tile([P, 2, N, 4], BF16, name="adj_g", align_bytes=64)
        c_g = keep.tile([P, 2, N, 4], BF16, name="c_g", align_bytes=64)
        x_g = keep.tile([P, 2, N, 4], BF16, name="x_g", align_bytes=64)
        y_g = keep.tile([P, 2, N, 4], BF16, name="y_g", align_bytes=64)
        adj_c = keep.tile([P, 2, N], U32, name="adj_c", align_bytes=64)
        c_c = keep.tile([P, 2, N], U32, name="c_c", align_bytes=64)
        x_c = keep.tile([P, 2, N], U32, name="x_c", align_bytes=64)
        y_c = keep.tile([P, 2, N], U32, name="y_c", align_bytes=64)
        adj_s = keep.tile([P, 2, N], U8, name="adj_s", align_bytes=64)
        c_s = keep.tile([P, 2, N], U8, name="c_s", align_bytes=64)
        x_s = keep.tile([P, 2, N], U8, name="x_s", align_bytes=64)
        y_s = keep.tile([P, 2, N], U8, name="y_s", align_bytes=64)
        V = nc.vector.tensor_copy
        S = nc.scalar.copy

        def quantise(grouped, codes, scales, g, c0, cols):
            nc.vector.quantize_mx(
                out=codes[:, g, c0:c0 + cols].bitcast(FP8X4),
                scales=scales[:, g, c0:c0 + cols],
                in_=grouped[:, g, c0:c0 + cols, :].rearrange("p j t -> p (j t)"),
            )

        def regroup(eng_copy, dst, src):
            eng_copy(out=dst.rearrange("p (c i) t -> p c t i", i=4),
                     in_=src.rearrange("p t (c i) -> p c t i", i=4))

        def a_cols(v, e, vc, ec):
            return a_sb[:, v, e, 256 * vc + ec:256 * vc + 256:2]

        rs = keep.tile([P, 16], F32, name="rs")
        live = {}

        def rowsum(w):
            nc.vector.tensor_reduce(out=rs[:, w:w + 1], in_=a_sb[:, w, 0, :], axis=AX.X, op=ALU.add)
            nc.scalar.activation(out=junk[:, w, :], in_=a_sb[:, w, 1, :], func=ACT.Copy,
                                 accum_out=rs[:, 8 + w:9 + w])

        def colsum_group(w, i):
            if w == 0 and i == 0:
                live["colp"] = bank(7, "colp")
            colp = live["colp"]
            i0 = (w * 8 + i) * 2
            e, v = i // 4, i % 4
            for ew in range(2):
                nc.tensor.matmul(colp[:, i0:i0 + 2], lhsT=a_cols(w, ew, v, e), rhs=ones_b[:],
                                 start=(ew == 0), stop=(ew == 1))

        def colsum(w, blocks):
            for i in range(8):
                colsum_group(w, i)
                if i % 2 == 1 and i // 2 < len(blocks):
                    n, t2 = blocks[i // 2]
                    add_blocks(n, t2, t2 + 1)

        def add_blocks(n, t_lo, t_hi):
            a, G, t0, b, col0 = TILES[n]
            v, e = a // 2, a % 2
            if t_lo == t0:
                live["s2p", n] = live["s2p", 4] if n == 6 else bank(b, "s2p")
            tl = live["s2p", n]
            for t2 in range(t_lo, t_hi):
                c = 4 * G + t2
                vc, ec = c // 2, c % 2
                o = tl[:, col0 + 128 * (t2 - t0):col0 + 128 * (t2 - t0 + 1)]
                nc.tensor.matmul(o, lhsT=ident_b[:], rhs=a_cols(v, e, vc, ec), start=True, stop=False)
                nc.tensor.matmul(o, lhsT=a_cols(vc, ec, v, e), rhs=ident_b[:], start=False, stop=(c != a))
                if c == a:
                    nc.tensor.matmul(o, lhsT=ident_b[:], rhs=two_eye[:], start=False, stop=True)

        def add_tile(n):
            add_blocks(n, TILES[n][2], 4)

        c_gw = c_g[:].bitcast(F32)

        def c_tr(ib, b):
            ctp = bank(b, "ctp")
            live["ctp", ib] = ctp
            for vv in range(4):
                nc.tensor.transpose(
                    ctp[:, 128 * vv:128 * (vv + 1)],
                    c_sb[:, ib, :].bitcast(F32)[:, 128 * vv:128 * (vv + 1)],
                    ident_f[:])

        def c_ev(ib, eng):
            eng(out=c_gw[:, :, 128 * ib:128 * (ib + 1), :],
                in_=live["ctp", ib][:].rearrange("p (g u i) -> p g i u", g=2, u=2))

        def small(name):
            return keep.tile([P, 8], F32, name=name)

        cs, d, dm, mask, rt, y0 = small("cs"), small("d"), small("dm"), small("mask"), small("rt"), small("y0")
        t1, t2s, y1, t3, y1m, t4, dinv = (small("t1"), small("t2s"), small("y1"), small("t3"), small("y1m"),
                                          small("t4"), small("dinv"))

        def chain_a():
            nc.vector.tensor_reduce(
                out=cs[:], in_=live["colp"][:, 0:64].rearrange("p (w a n) -> p a n w", w=4, n=2)[:, :, 0, :],
                axis=AX.X, op=ALU.add)
            nc.vector.scalar_tensor_tensor(
                out=d[:].rearrange("p (e v) -> p e v", e=2),
                in0=rs[:].rearrange("p (e c) -> p e c", e=2)[:, :, 0:4], scalar=2.0,
                in1=cs[:].rearrange("p (e v) -> p e v", e=2), op0=ALU.add, op1=ALU.add)
            nc.vector.tensor_scalar_max(out=dm[:], in0=d[:], scalar1=TINY)
            nc.scalar.activation(out=rt[:], in_=dm[:], func=ACT.Sqrt)
            nc.vector.tensor_single_scalar(out=mask[:], in_=d[:], scalar=0.0, op=ALU.is_gt)

        def chain_b():
            stt = nc.vector.scalar_tensor_tensor
            nc.vector.reciprocal(out=y0[:], in_=rt[:])
            nc.vector.tensor_mul(out=t1[:], in0=dm[:], in1=y0[:])
            stt(out=t2s[:], in0=t1[:], scalar=-0.5, in1=y0[:], op0=ALU.mult, op1=ALU.mult)
            stt(out=y1[:], in0=t2s[:], scalar=1.5, in1=y0[:], op0=ALU.add, op1=ALU.mult)
            nc.vector.tensor_mul(out=t3[:], in0=dm[:], in1=y1[:])
            nc.vector.tensor_mul(out=y1m[:], in0=y1[:], in1=mask[:])
            stt(out=t4[:], in0=t3[:], scalar=-0.5, in1=y1[:], op0=ALU.mult, op1=ALU.mult)
            stt(out=dinv[:], in0=t4[:], scalar=1.5, in1=y1m[:], op0=ALU.add, op1=ALU.mult)

        def dcol(a):
            i = 4 * (a % 2) + a // 2
            return dinv[:, i:i + 1]

        def bcast(g, b, eng):
            rowp = bank(b, "rowp")
            for t in range(4):
                nc.tensor.transpose(rowp[:, 128 * t:128 * (t + 1)], dcol(4 * g + t).to_broadcast([P, P]), ident_f[:])
            eng(out=dj_sb[:, 512 * g:512 * (g + 1)], in_=rowp[:])

        def scale_tile(n):
            a, G, t0, b, col0 = TILES[n]
            lo, hi = 512 * G + 128 * t0, 512 * (G + 1)
            nc.vector.scalar_tensor_tensor(
                out=adjn[:, a, lo:hi], in0=live["s2p", n][:, col0:col0 + hi - lo], scalar=dcol(a),
                in1=dj_sb[:, lo:hi], op0=ALU.mult, op1=ALU.mult)

        def ld_tr(g, b):
            ld = bank_bf(b, "ld")
            live["ld", g] = ld
            for r in range(2):
                a = 4 * g + 2 + r
                for cc in range(2):
                    c = 4 * g + cc
                    q = 2 * r + cc
                    nc.tensor.transpose(ld[:, 128 * q:128 * (q + 1)], adjn[:, c, 128 * a:128 * (a + 1)], ident_b[:])

        def ld_ev(g, eng):
            eng(out=adjn[:, 4 * g + 2:4 * g + 4, 512 * g:512 * g + 256],
                in_=live["ld", g][:, 0:512].rearrange("p (r j) -> p r j", r=2))

        def lt_tr(h, b):
            lt = bank_bf(b, "lt")
            live["lt", h] = lt
            for cl in range(2):
                c = 2 * h + cl
                for t in range(4):
                    q = 4 * cl + t
                    nc.tensor.transpose(lt[:, 128 * q:128 * (q + 1)], adjn[:, c, 128 * (4 + t):128 * (5 + t)],
                                        ident_b[:])

        def lt_ev(h, eng):
            eng(out=adj_g[:, 1, 256 * h:256 * (h + 1), :].rearrange("p (cl j) t -> p cl j t", cl=2),
                in_=live["lt", h][:].rearrange("p (cl t j) -> p cl j t", cl=2, t=4))

        def rg_adj(g, c0, cols, eng):
            regroup(eng, adj_g[:, g, c0:c0 + cols, :], adjn[:, 4 * g:4 * g + 4, c0:c0 + cols])

        def q_adj(g, c0, cols):
            quantise(adj_g, adj_c, adj_s, g, c0, cols)

        def m1(G, ib, b, t_lo, t_hi):
            if t_lo == 0:
                live["yp", G, ib] = bank(b, "yp")
            yp = live["yp", G, ib]
            for t2 in range(t_lo, t_hi):
                j0 = 512 * G + 128 * t2
                for g in range(2):
                    nc.tensor.matmul_mx(
                        out=yp[:, 128 * t2:128 * (t2 + 1)],
                        lhsT=adj_c[:, g, j0:j0 + 128].bitcast(FP8X4),
                        lhsT_scale=adj_s[:, g, j0:j0 + 128],
                        rhs=c_c[:, g, 128 * ib:128 * (ib + 1)].bitcast(FP8X4),
                        rhs_scale=c_s[:, g, 128 * ib:128 * (ib + 1)],
                        start=(g == 0), stop=(g == 1))

        def y_ev(G, ib, eng):
            eng(out=y_g[:, G, 128 * ib:128 * (ib + 1), :],
                in_=live["yp", G, ib][:].rearrange("p (t i) -> p i t", t=4))

        def x_rg(G, c0, cols, eng):
            regroup(eng, x_g[:, G, c0:c0 + cols, :], x_sb[:, G, :, c0:c0 + cols])

        def m2(ib, h, b):
            op = bank(b, "op")
            live["op", ib, h] = op
            for G in range(2):
                nc.tensor.matmul_mx(
                    out=op[:],
                    lhsT=y_c[:, G, 128 * ib:128 * (ib + 1)].bitcast(FP8X4),
                    lhsT_scale=y_s[:, G, 128 * ib:128 * (ib + 1)],
                    rhs=x_c[:, G, 512 * h:512 * (h + 1)].bitcast(FP8X4),
                    rhs_scale=x_s[:, G, 512 * h:512 * (h + 1)],
                    start=(G == 0), stop=(G == 1))

        def o_ev(ib, h, eng):
            ost = stage.tile([P, 512], F32, name="ost")
            eng(out=ost[:], in_=live["op", ib, h][:])
            nc.sync.dma_start(out=out[128 * ib:128 * (ib + 1), 512 * h:512 * (h + 1)], in_=ost[:])

        for w in range(4):
            colsum(w, [])
            rowsum(w)
        chain_a()
        c_tr(0, 5)
        c_ev(0, S)
        add_tile(0)
        c_tr(1, 6)
        c_ev(1, S)
        add_tile(2)
        c_tr(2, 5)
        c_ev(2, S)
        c_tr(3, 6)
        c_ev(3, S)
        add_tile(4)
        chain_b()
        quantise(c_g, c_c, c_s, 0, 0, 256)
        quantise(c_g, c_c, c_s, 1, 0, 256)
        bcast(0, 7, V)
        add_tile(6)
        add_tile(1)
        bcast(1, 7, S)
        add_tile(3)
        scale_tile(0)
        scale_tile(2)
        add_tile(5)
        ld_tr(0, 5)
        ld_ev(0, S)
        scale_tile(4)
        scale_tile(6)
        add_tile(7)
        c_tr(4, 6)
        c_ev(4, S)
        scale_tile(1)
        scale_tile(3)
        lt_tr(0, 7)
        lt_ev(0, S)
        add_tile(8)
        c_tr(5, 5)
        c_ev(5, S)
        scale_tile(5)
        scale_tile(7)
        lt_tr(1, 6)
        lt_ev(1, S)
        add_tile(9)
        c_tr(6, 5)
        c_ev(6, S)
        add_tile(10)
        c_tr(7, 7)
        c_ev(7, S)
        add_tile(11)
        rg_adj(0, 0, 512, V)
        quantise(c_g, c_c, c_s, 0, 256, 256)
        q_adj(0, 0, 512)
        quantise(c_g, c_c, c_s, 1, 256, 256)
        q_adj(1, 0, 512)
        scale_tile(8)
        scale_tile(9)
        quantise(c_g, c_c, c_s, 0, 512, 512)
        quantise(c_g, c_c, c_s, 1, 512, 512)
        scale_tile(10)
        scale_tile(11)
        rg_adj(1, 512, 512, V)
        YB0 = [6, 7, 5, 2, 4, 1, 3, 0]
        for ib in range(8):
            m1(0, ib, YB0[ib], 0, 4)
            y_ev(0, ib, S)
            if ib in (0, 2):
                rg_adj(0, 512 + 128 * ib, 256, S)
            if ib == 2:
                q_adj(1, 512, 512)
                q_adj(0, 512, 512)
                x_rg(0, 0, 512, V)
                x_rg(1, 0, 512, V)
                quantise(x_g, x_c, x_s, 0, 0, 512)
                quantise(x_g, x_c, x_s, 1, 0, 512)
        quantise(y_g, y_c, y_s, 0, 0, 512)
        quantise(y_g, y_c, y_s, 0, 512, 512)
        for ib in range(8):
            m1(1, ib, YB0[ib], 0, 4)
            y_ev(1, ib, S)
            if ib % 2 == 1:
                quantise(y_g, y_c, y_s, 1, 128 * (ib - 1), 256)
            if ib == 5:
                x_rg(0, 512, 512, V)
        x_rg(1, 512, 512, V)
        quantise(x_g, x_c, x_s, 0, 512, 512)
        quantise(x_g, x_c, x_s, 1, 512, 512)
        for ib in range(8):
            m2(ib, 0, YB0[ib])
            o_ev(ib, 0, S)
        for ib in range(8):
            m2(ib, 1, YB0[ib])
            o_ev(ib, 1, V if ib % 2 == 0 else S)
